import numpy as np
import ml_dtypes


def mxq(x, axis, fmt="e4m3"):
    dtype, down = {"e4m3": (ml_dtypes.float8_e4m3fn, 7), "e5m2": (ml_dtypes.float8_e5m2, 14)}[fmt]
    v = np.moveaxis(np.asarray(x, np.float32).astype(ml_dtypes.bfloat16).astype(np.float64), axis, -1)
    blocks = v.reshape(v.shape[:-1] + (-1, 32))
    amax = np.abs(blocks).max(-1, keepdims=True)
    byte = np.maximum(np.where(amax > 0, np.frexp(amax)[1] - 1 + 127, 0) - down, 1)
    scale = np.exp2(byte - 127.0)
    codes = (blocks / scale).astype(np.float32).astype(dtype).astype(np.float64)
    return np.moveaxis((codes * scale).reshape(v.shape), -1, axis)


WIDE = False


def mx_kscale(k):
    if not WIDE:
        return np.ones(k)
    levels = np.array([10, -10, 5, -5, 0])
    a = np.random.permutation(np.resize(levels, k // 512 * 4)).reshape(k // 512, 4)
    idx = np.arange(k)
    return np.exp2(a[idx // 512, idx % 128 // 32])


BF16 = ml_dtypes.bfloat16


def bf(x):
    return np.asarray(x, np.float32).astype(BF16)


def f64(x):
    return np.asarray(x).astype(np.float64)


B, T, C, H, H_KV, QB = 1, 1024, 1536, 12, 6, 512
D = C // H
G = H // H_KV
NB = T // QB


def setup_inputs():
    t = mx_kscale(C).reshape(H_KV, G, D)[:, 0, :]
    tp = np.repeat(t, G, axis=0).reshape(C)
    return {"q_rot": bf(np.random.standard_normal((B, H, T, D))),
            "k_rot": bf(np.random.standard_normal((B, H_KV, T, D))),
            "v": bf(np.square(np.random.standard_normal((B, H_KV, T, D))) * 1.2 * t[None, :, None, :]),
            "Wp": bf(np.random.standard_normal((C, C)) * 2.0 / np.sqrt(C) / tp[:, None])}


def reference(q_rot, k_rot, v, Wp):
    qg = f64(q_rot).reshape(B, H_KV, G, T, D)
    kt = f64(k_rot).transpose(0, 1, 3, 2)
    vq = mxq(f64(v), 2, "e4m3")
    rows = []
    for i in range(NB):
        n = (i + 1) * QB
        s = qg[:, :, :, i * QB:n].reshape(B, H_KV, G * QB, D) @ kt[:, :, :, :n] / np.sqrt(D)
        keep = np.arange(n)[None, :] <= np.arange(i * QB, n)[:, None]
        s = np.where(keep, s.reshape(B, H_KV, G, QB, n), -np.inf)
        e = np.exp(s - s.max(-1, keepdims=True))
        ev = mxq(e.reshape(B, H_KV, G * QB, n), 3, "e4m3") @ vq[:, :, :n]
        rows.append(ev.reshape(B, H_KV, G, QB, D) / e.sum(-1, keepdims=True))
    o = np.concatenate(rows, axis=3).reshape(B, H, T, D)
    a = o.transpose(0, 2, 1, 3).reshape(B, T, C)
    return mxq(a, 2, "e4m3") @ mxq(f64(Wp), 0, "e4m3")

@@ -1,0 +1,443 @@
+from contextlib import ExitStack
+import math
+
+import concourse.mybir as mybir
+from concourse.masks import make_identity
+
+F32 = mybir.dt.float32
+BF16 = mybir.dt.bfloat16
+U32 = mybir.dt.uint32
+U8 = mybir.dt.uint8
+FP8X4 = mybir.dt.float8_e4m3fn_x4
+ALU = mybir.AluOpType
+ACT = mybir.ActivationFunctionType
+AX = mybir.AxisListType
+
+P = 128
+PACK = 4
+K_PASS = P * PACK
+T = 1024
+D = 128
+H = 12
+H_KV = 6
+C = H * D
+N_TILE = 512
+Q_TILES = T // P
+KEY_PASSES = T // K_PASS
+C_PASSES = C // K_PASS
+N_TILES = C // N_TILE
+TILES_PER_PASS = K_PASS // P
+HEADS_PER_GROUP = K_PASS // D
+SCALE = 1.0 / math.sqrt(D)
+MASKED = -1.0e30
+
+FLOPS = 2 * 2 * H * (512 * 512 + 512 * 1024) * D + 2 * T * C * C
+
+E_BUFS = 4
+CODE_BUFS = 8
+LAG_TRANSPOSE = 2
+LAG_QUANTISE = 3
+LAG_PV = 4
+LAG_NORMALISE = 5
+LAG_A_TRANSPOSE = 6
+LAG_A_QUANTISE = 7
+LAG_PROJECT = 8
+WP_CHUNKS = C_PASSES * N_TILES
+V_LATE_START = WP_CHUNKS + 1
+
+
+def tile_gqa_pb_kernel(tc, q_rot, k_rot, v, Wp, out):
+    nc = tc.nc
+
+    works = []
+    for qi in range(Q_TILES):
+        heads_per_work = 2 if qi < TILES_PER_PASS else 1
+        for first_head in range(0, H, heads_per_work):
+            works.append((qi, first_head, heads_per_work))
+    n_works = len(works)
+
+    def half_of(w, c):
+        qi, first_head, heads_per_work = works[w]
+        n_keys = P * (qi + 1)
+        if heads_per_work == 2:
+            return first_head + c, 0, n_keys
+        return first_head, K_PASS * c, (K_PASS if c == 0 else n_keys - K_PASS)
+
+    def is_work(w):
+        return 0 <= w < n_works
+
+    def ends_group(w):
+        return is_work(w) and (works[w][1] + works[w][2]) % HEADS_PER_GROUP == 0
+
+    def ends_tile(w):
+        return is_work(w) and works[w][1] + works[w][2] == H
+
+    with ExitStack() as stack:
+        keep = stack.enter_context(tc.tile_pool(name="keep", bufs=1))
+        ring = stack.enter_context(tc.tile_pool(name="ring", bufs=2))
+        small = stack.enter_context(tc.tile_pool(name="small", bufs=4))
+        psum_s = stack.enter_context(tc.psum_pool(name="psum_s", bufs=4))
+        psum_tr = stack.enter_context(tc.psum_pool(name="psum_tr", bufs=2))
+        psum_acc = stack.enter_context(tc.psum_pool(name="psum_acc", bufs=2))
+
+        q_view = q_rot[0].rearrange("h (n p) d -> n p h d", p=P)
+        k_view = k_rot[0].rearrange("j (n p) d -> n p j d", p=P)
+        v_view = v[0].rearrange("j (g u p e) d -> g u p j (e d)", g=KEY_PASSES, u=2, p=P, e=2)
+        wp_view = Wp.rearrange("(g u p e) n -> g u p (e n)", g=C_PASSES, u=2, p=P, e=2)
+        q_raw = []
+        k_raw = []
+        for qi in range(Q_TILES):
+            q_raw.append(keep.tile([P, H, D], BF16, name="q_raw%d" % qi))
+            k_raw.append(keep.tile([P, H_KV, D], BF16, name="k_raw%d" % qi))
+        v_raw = keep.tile([P, KEY_PASSES, H_KV, PACK, D], BF16)
+        wp_raw = keep.tile([P, C_PASSES, PACK, C], BF16)
+
+        def load_qk(qi):
+            nc.sync.dma_start(out=q_raw[qi][:], in_=q_view[qi])
+            nc.sync.dma_start(out=k_raw[qi][:], in_=k_view[qi])
+
+        def load_v(g):
+            for u in range(2):
+                nc.sync.dma_start(
+                    out=v_raw[:, g, :, 2 * u : 2 * u + 2, :].rearrange("p j e d -> p j (e d)"),
+                    in_=v_view[g, u],
+                )
+
+        def load_wp(g):
+            for u in range(2):
+                nc.sync.dma_start(
+                    out=wp_raw[:, g, 2 * u : 2 * u + 2, :].rearrange("p e n -> p (e n)"),
+                    in_=wp_view[g, u],
+                )
+
+        load_qk(0)
+        load_v(0)
+        load_qk(1)
+        load_wp(0)
+        load_qk(2)
+        load_wp(1)
+        load_wp(2)
+        load_v(1)
+        for qi in range(3, Q_TILES):
+            load_qk(qi)
+
+        ident_bf = keep.tile([P, P], BF16)
+        make_identity(nc, ident_bf[:])
+        ident_f32 = keep.tile([P, P], F32)
+        make_identity(nc, ident_f32[:])
+        mask_f32 = keep.tile([P, P], F32)
+        nc.gpsimd.memset(mask_f32[:], 0.0)
+        nc.gpsimd.affine_select(
+            out=mask_f32[:],
+            in_=mask_f32[:],
+            compare_op=ALU.is_ge,
+            fill=MASKED,
+            base=0,
+            pattern=[[-1, P]],
+            channel_multiplier=1,
+        )
+        mask_bf = keep.tile([P, P], BF16)
+        nc.vector.tensor_copy(out=mask_bf[:], in_=mask_f32[:])
+        warm_in = keep.tile([P, 1], F32)
+        warm_out = keep.tile([P, 1], F32)
+        nc.vector.memset(warm_in[:], 0.0)
+        nc.scalar.activation(out=warm_out[:], in_=warm_in[:], func=ACT.Exp)
+
+        e_tiles = []
+        for block in range(2):
+            row = []
+            for b in range(E_BUFS):
+                e_tile = keep.tile([P, 2, K_PASS], BF16, name="e%d_%d" % (block, b))
+                nc.vector.memset(e_tile[:], 0.0)
+                row.append(e_tile)
+            e_tiles.append(row)
+
+        def e_of(w):
+            return e_tiles[0 if works[w][2] == 2 else 1][w % E_BUFS]
+
+        kT = keep.tile([P, H_KV, T], BF16)
+        v_codes = keep.tile([P, KEY_PASSES, H_KV, D], U32, align_bytes=64)
+        v_scales = keep.tile([P, KEY_PASSES, H_KV, D], U8, align_bytes=64)
+        wp_codes = keep.tile([P, C_PASSES, C], U32, align_bytes=64)
+        wp_scales = keep.tile([P, C_PASSES, C], U8, align_bytes=64)
+
+        qT = {}
+        s_banks = {}
+        neg_max = {}
+        row_sums = {}
+        e_grouped = {}
+        e_codes = {}
+        e_scales = {}
+        pv_banks = {}
+        a_tiles = {}
+        a_grouped = {}
+        a_codes = {}
+        a_scales = {}
+        wp_grouped = {}
+
+        def prepare_v(g, pair):
+            grouped = ring.tile([P, 2, D, PACK], BF16, align_bytes=64, tag="v_grouped")
+            for i in range(2):
+                nc.vector.tensor_copy(
+                    out=grouped[:, i, :, :],
+                    in_=v_raw[:, g, 2 * pair + i, :, :].rearrange("p t d -> p d t"),
+                )
+            heads = slice(2 * pair, 2 * pair + 2)
+            nc.vector.quantize_mx(
+                out=v_codes[:, g, heads, :].rearrange("p j d -> p (j d)").bitcast(FP8X4),
+                scales=v_scales[:, g, heads, :].rearrange("p j d -> p (j d)"),
+                in_=grouped[:].rearrange("p j d t -> p (j d t)"),
+            )
+
+        def regroup_wp(chunk):
+            g, nt = divmod(chunk, N_TILES)
+            grouped = ring.tile([P, N_TILE, PACK], BF16, align_bytes=64, tag="wp_grouped")
+            nc.vector.tensor_copy(
+                out=grouped[:].rearrange("p (c i) t -> p c t i", i=4),
+                in_=wp_raw[:, g, :, N_TILE * nt : N_TILE * (nt + 1)].rearrange(
+                    "p t (c i) -> p c t i", i=4
+                ),
+            )
+            wp_grouped[chunk] = grouped
+
+        def quantise_wp(chunk):
+            g, nt = divmod(chunk, N_TILES)
+            cols = slice(N_TILE * nt, N_TILE * (nt + 1))
+            nc.vector.quantize_mx(
+                out=wp_codes[:, g, cols].bitcast(FP8X4),
+                scales=wp_scales[:, g, cols],
+                in_=wp_grouped[chunk][:].rearrange("p n t -> p (n t)"),
+            )
+
+        def transpose_qk(qi, part):
+            if part == 0:
+                qT_tile = ring.tile([P, H, P], BF16, tag="qT")
+                qT[qi] = qT_tile
+            xt = psum_tr.tile([P, H_KV, P], BF16, tag="tr")
+            for i in range(H_KV):
+                src = k_raw[qi][:, i, :] if part == 2 else q_raw[qi][:, H_KV * part + i, :]
+                nc.tensor.transpose(xt[:, i, :], src, ident_bf[:])
+            if part == 2:
+                nc.scalar.copy(out=kT[:, :, P * qi : P * (qi + 1)], in_=xt[:])
+            else:
+                nc.scalar.copy(out=qT[qi][:, H_KV * part : H_KV * (part + 1), :], in_=xt[:])
+
+        def scores(w):
+            qi = works[w][0]
+            banks = []
+            for c in range(2):
+                head, key0, n_keys = half_of(w, c)
+                s = psum_s.tile([P, N_TILE], F32, tag="s")
+                on_diagonal = key0 + n_keys == P * (qi + 1)
+                nc.tensor.matmul(
+                    out=s[:, 0:n_keys],
+                    lhsT=qT[qi][:, head, :],
+                    rhs=kT[:, head // 2, key0 : key0 + n_keys],
+                    start=True,
+                    stop=not on_diagonal,
+                )
+                if on_diagonal:
+                    nc.tensor.matmul(
+                        out=s[:, n_keys - P : n_keys],
+                        lhsT=ident_bf[:],
+                        rhs=mask_bf[:],
+                        start=False,
+                        stop=True,
+                    )
+                banks.append(s)
+            s_banks[w] = banks
+
+        def row_max(w):
+            heads_per_work = works[w][2]
+            largest = small.tile([P, 2], F32, tag="largest")
+            for c in range(2):
+                n_keys = half_of(w, c)[2]
+                nc.vector.reduce_max(out=largest[:, c : c + 1], in_=s_banks[w][c][:, 0:n_keys], axis=AX.X)
+            bias = small.tile([P, 2], F32, tag="bias")
+            if heads_per_work == 2:
+                nc.vector.tensor_scalar(
+                    out=bias[:], in0=largest[:], scalar1=-SCALE, scalar2=None, op0=ALU.mult
+                )
+            else:
+                nc.vector.tensor_scalar(
+                    out=bias[:, 0:1],
+                    in0=largest[:, 0:1],
+                    scalar1=largest[:, 1:2],
+                    scalar2=-SCALE,
+                    op0=ALU.max,
+                    op1=ALU.mult,
+                )
+            neg_max[w] = bias
+
+        def exponentials(w):
+            qi, first_head, heads_per_work = works[w]
+            if first_head == 0:
+                sums = ring.tile([P, H, 2], F32, tag="row_sums")
+                row_sums[qi] = sums
+            for c in range(2):
+                head, key0, n_keys = half_of(w, c)
+                col = c if heads_per_work == 2 else 0
+                part = 0 if heads_per_work == 2 else c
+                nc.scalar.activation(
+                    out=e_of(w)[:, c, 0:n_keys],
+                    in_=s_banks[w][c][:, 0:n_keys],
+                    func=ACT.Exp,
+                    bias=neg_max[w][:, col : col + 1],
+                    scale=SCALE,
+                    accum_out=row_sums[qi][:, head, part : part + 1],
+                )
+
+        def transpose_e(w):
+            e_words = e_of(w)[:].bitcast(F32)
+            xt = psum_tr.tile([P, 4, P], F32, tag="tr")
+            for c in range(2):
+                for u in range(2):
+                    nc.tensor.transpose(
+                        xt[:, 2 * c + u, :], e_words[:, c, P * u : P * (u + 1)], ident_f32[:]
+                    )
+            grouped = ring.tile([P, 2 * K_PASS], BF16, align_bytes=64, tag="e_grouped", bufs=3)
+            nc.scalar.copy(
+                out=grouped[:].bitcast(F32).rearrange("p (c q u) -> p c q u", c=2, u=2),
+                in_=xt[:].rearrange("p (c u) q -> p c q u", u=2),
+            )
+            e_grouped[w] = grouped
+
+        def quantise_e(w):
+            codes = ring.tile([P, 2, P], U32, align_bytes=64, tag="e_codes", bufs=CODE_BUFS)
+            scales = ring.tile([P, 2, P], U8, align_bytes=64, tag="e_scales", bufs=CODE_BUFS)
+            nc.vector.quantize_mx(
+                out=codes[:].rearrange("p c q -> p (c q)").bitcast(FP8X4),
+                scales=scales[:].rearrange("p c q -> p (c q)"),
+                in_=e_grouped[w][:],
+            )
+            e_codes[w] = codes
+            e_scales[w] = scales
+
+        def group_works(last):
+            return range(last + 1 - HEADS_PER_GROUP // works[last][2], last + 1)
+
+        def e_times_v(last):
+            pv = psum_acc.tile([P, HEADS_PER_GROUP, D], F32, tag="acc")
+            for w in group_works(last):
+                lone = works[w][2] == 2
+                for c in range(2):
+                    head, key0, n_keys = half_of(w, c)
+                    g = key0 // K_PASS
+                    nc.tensor.matmul_mx(
+                        out=pv[:, head % HEADS_PER_GROUP, :],
+                        lhsT=e_codes[w][:, c, :].bitcast(FP8X4),
+                        lhsT_scale=e_scales[w][:, c, :],
+                        rhs=v_codes[:, g, head // 2, :].bitcast(FP8X4),
+                        rhs_scale=v_scales[:, g, head // 2, :],
+                        start=lone or c == 0,
+                        stop=lone or c == 1,
+                    )
+            pv_banks[last] = pv
+
+        def normalise(last):
+            qi, first_head, heads_per_work = works[last]
+            group = (first_head + heads_per_work) // HEADS_PER_GROUP - 1
+            heads = slice(HEADS_PER_GROUP * group, HEADS_PER_GROUP * (group + 1))
+            if group == 0:
+                a_tile = ring.tile([P, H, D], BF16, tag="a")
+                a_tiles[qi] = a_tile
+            inverse = small.tile([P, HEADS_PER_GROUP], F32, tag="inverse")
+            if heads_per_work == 2:
+                nc.vector.reciprocal(out=inverse[:], in_=row_sums[qi][:, heads, 0])
+            else:
+                total = small.tile([P, HEADS_PER_GROUP], F32, tag="total")
+                nc.vector.reduce_sum(out=total[:], in_=row_sums[qi][:, heads, :], axis=AX.X)
+                nc.vector.reciprocal(out=inverse[:], in_=total[:])
+            nc.vector.tensor_tensor(
+                out=a_tiles[qi][:, heads, :],
+                in0=pv_banks[last][:],
+                in1=inverse[:].unsqueeze(2).to_broadcast([P, HEADS_PER_GROUP, D]),
+                op=ALU.mult,
+            )
+
+        def transpose_a(qi):
+            a_words = a_tiles[qi][:].rearrange("p h d -> p (h d)").bitcast(F32)
+            grouped = ring.tile([P, C_PASSES * K_PASS], BF16, align_bytes=64, tag="a_grouped")
+            for first_pass, n_passes in ((0, 2), (2, 1)):
+                xt = psum_tr.tile([P, 4, P], F32, tag="tr")
+                for i in range(2 * n_passes):
+                    word0 = 2 * P * first_pass + P * i
+                    nc.tensor.transpose(xt[:, i, :], a_words[:, word0 : word0 + P], ident_f32[:])
+                nc.vector.tensor_copy(
+                    out=grouped[:, K_PASS * first_pass : K_PASS * (first_pass + n_passes)]
+                    .bitcast(F32)
+                    .rearrange("p (c q u) -> p c q u", c=n_passes, u=2),
+                    in_=xt[:, 0 : 2 * n_passes, :].rearrange("p (c u) q -> p c q u", u=2),
+                )
+            a_grouped[qi] = grouped
+
+        def quantise_a(qi):
+            codes = ring.tile([P, C_PASSES, P], U32, align_bytes=64, tag="a_codes")
+            scales = ring.tile([P, C_PASSES, P], U8, align_bytes=64, tag="a_scales")
+            for first_pass, n_passes in ((0, 2), (2, 1)):
+                passes = slice(first_pass, first_pass + n_passes)
+                nc.vector.quantize_mx(
+                    out=codes[:, passes, :].rearrange("p c q -> p (c q)").bitcast(FP8X4),
+                    scales=scales[:, passes, :].rearrange("p c q -> p (c q)"),
+                    in_=a_grouped[qi][:, K_PASS * first_pass : K_PASS * (first_pass + n_passes)],
+                )
+            a_codes[qi] = codes
+            a_scales[qi] = scales
+
+        def project(qi):
+            result = ring.tile([P, C], F32, tag="result")
+            for nt in range(N_TILES):
+                cols = slice(N_TILE * nt, N_TILE * (nt + 1))
+                acc = psum_acc.tile([P, N_TILE], F32, tag="acc")
+                for g in range(C_PASSES):
+                    nc.tensor.matmul_mx(
+                        out=acc[:],
+                        lhsT=a_codes[qi][:, g, :].bitcast(FP8X4),
+                        lhsT_scale=a_scales[qi][:, g, :],
+                        rhs=wp_codes[:, g, cols].bitcast(FP8X4),
+                        rhs_scale=wp_scales[:, g, cols],
+                        start=(g == 0),
+                        stop=(g == C_PASSES - 1),
+                    )
+                nc.scalar.copy(out=result[:, cols], in_=acc[:])
+                nc.sync.dma_start(out=out[0, P * qi : P * (qi + 1), cols], in_=result[:, cols])
+
+        for part in range(3):
+            transpose_qk(0, part)
+        for pair in range(H_KV // 2):
+            prepare_v(0, pair)
+
+        first_work_of_tile = 0
+        for w in range(n_works + LAG_PROJECT + 1):
+            if is_work(w):
+                qi = works[w][0]
+                if works[w][1] == 0:
+                    first_work_of_tile = w
+                scores(w)
+            if is_work(w - LAG_QUANTISE):
+                quantise_e(w - LAG_QUANTISE)
+            if is_work(w):
+                row_max(w)
+            if is_work(w - LAG_TRANSPOSE):
+                transpose_e(w - LAG_TRANSPOSE)
+            if is_work(w):
+                part = w - first_work_of_tile
+                if part < 3 and qi + 1 < Q_TILES:
+                    transpose_qk(qi + 1, part)
+                exponentials(w)
+            if w < WP_CHUNKS:
+                regroup_wp(w)
+            if 1 <= w <= WP_CHUNKS:
+                quantise_wp(w - 1)
+            if 0 <= w - V_LATE_START < H_KV // 2:
+                prepare_v(1, w - V_LATE_START)
+            if ends_group(w - LAG_PV):
+                e_times_v(w - LAG_PV)
+            if ends_group(w - LAG_NORMALISE):
+                normalise(w - LAG_NORMALISE)
+            if ends_tile(w - LAG_A_TRANSPOSE):
+                transpose_a(works[w - LAG_A_TRANSPOSE][0])
+            if ends_tile(w - LAG_A_QUANTISE):
+                quantise_a(works[w - LAG_A_QUANTISE][0])
+            if ends_tile(w - LAG_PROJECT):
+                project(works[w - LAG_PROJECT][0])

@@ -11,7 +11,6 @@ U8 = mybir.dt.uint8
 FP8X4 = mybir.dt.float8_e4m3fn_x4
 ALU = mybir.AluOpType
 ACT = mybir.ActivationFunctionType
-AX = mybir.AxisListType
 
 P = 128
 PACK = 4
@@ -34,6 +33,7 @@ MASKED = -1.0e30
 FLOPS = 2 * 2 * H * (512 * 512 + 512 * 1024) * D + 2 * T * C * C
 
 E_BUFS = 4
+SCALED_BUFS = 4
 CODE_BUFS = 8
 LAG_TRANSPOSE = 2
 LAG_QUANTISE = 3
@@ -76,8 +76,8 @@ def tile_gqa_pb_kernel(tc, q_rot, k_rot, v, Wp, out):
         keep = stack.enter_context(tc.tile_pool(name="keep", bufs=1))
         ring = stack.enter_context(tc.tile_pool(name="ring", bufs=2))
         small = stack.enter_context(tc.tile_pool(name="small", bufs=4))
-        psum_s = stack.enter_context(tc.psum_pool(name="psum_s", bufs=4))
-        psum_tr = stack.enter_context(tc.psum_pool(name="psum_tr", bufs=2))
+        psum_s = stack.enter_context(tc.psum_pool(name="psum_s", bufs=3))
+        psum_tr = stack.enter_context(tc.psum_pool(name="psum_tr", bufs=3))
         psum_acc = stack.enter_context(tc.psum_pool(name="psum_acc", bufs=2))
 
         q_view = q_rot[0].rearrange("h (n p) d -> n p h d", p=P)
@@ -163,6 +163,7 @@ def tile_gqa_pb_kernel(tc, q_rot, k_rot, v, Wp, out):
 
         qT = {}
         s_banks = {}
+        scaled_scores = {}
         neg_max = {}
         row_sums = {}
         e_grouped = {}
@@ -249,25 +250,28 @@ def tile_gqa_pb_kernel(tc, q_rot, k_rot, v, Wp, out):
 
         def row_max(w):
             heads_per_work = works[w][2]
-            largest = small.tile([P, 2], F32, tag="largest")
+            scaled = ring.tile([P, 2, N_TILE], F32, tag="scaled", bufs=SCALED_BUFS)
+            bias = small.tile([P, 2], F32, tag="bias")
             for c in range(2):
                 n_keys = half_of(w, c)[2]
-                nc.vector.reduce_max(out=largest[:, c : c + 1], in_=s_banks[w][c][:, 0:n_keys], axis=AX.X)
-            bias = small.tile([P, 2], F32, tag="bias")
+                nc.vector.tensor_scalar(
+                    out=scaled[:, c, 0:n_keys],
+                    in0=s_banks[w][c][:, 0:n_keys],
+                    scalar1=-SCALE,
+                    scalar2=None,
+                    op0=ALU.mult,
+                    op1=ALU.min,
+                    accum_out=bias[:, c : c + 1],
+                )
+            scaled_scores[w] = scaled
             if heads_per_work == 2:
-                nc.vector.tensor_scalar(
-                    out=bias[:], in0=largest[:], scalar1=-SCALE, scalar2=None, op0=ALU.mult
-                )
+                neg_max[w] = (bias[:, 0:1], bias[:, 1:2])
             else:
-                nc.vector.tensor_scalar(
-                    out=bias[:, 0:1],
-                    in0=largest[:, 0:1],
-                    scalar1=largest[:, 1:2],
-                    scalar2=-SCALE,
-                    op0=ALU.max,
-                    op1=ALU.mult,
+                joined = small.tile([P, 1], F32, tag="joined")
+                nc.gpsimd.tensor_scalar(
+                    out=joined[:], in0=bias[:, 0:1], scalar1=bias[:, 1:2], scalar2=None, op0=ALU.min
                 )
-            neg_max[w] = bias
+                neg_max[w] = (joined[:], joined[:])
 
         def exponentials(w):
             qi, first_head, heads_per_work = works[w]
@@ -276,14 +280,13 @@ def tile_gqa_pb_kernel(tc, q_rot, k_rot, v, Wp, out):
                 row_sums[qi] = sums
             for c in range(2):
                 head, key0, n_keys = half_of(w, c)
-                col = c if heads_per_work == 2 else 0
                 part = 0 if heads_per_work == 2 else c
                 nc.scalar.activation(
                     out=e_of(w)[:, c, 0:n_keys],
-                    in_=s_banks[w][c][:, 0:n_keys],
+                    in_=scaled_scores[w][:, c, 0:n_keys],
                     func=ACT.Exp,
-                    bias=neg_max[w][:, col : col + 1],
-                    scale=SCALE,
+                    bias=neg_max[w][c],
+                    scale=-1.0,
                     accum_out=row_sums[qi][:, head, part : part + 1],
                 )
 
@@ -346,7 +349,12 @@ def tile_gqa_pb_kernel(tc, q_rot, k_rot, v, Wp, out):
                 nc.vector.reciprocal(out=inverse[:], in_=row_sums[qi][:, heads, 0])
             else:
                 total = small.tile([P, HEADS_PER_GROUP], F32, tag="total")
-                nc.vector.reduce_sum(out=total[:], in_=row_sums[qi][:, heads, :], axis=AX.X)
+                nc.gpsimd.tensor_tensor(
+                    out=total[:],
+                    in0=row_sums[qi][:, heads, 0],
+                    in1=row_sums[qi][:, heads, 1],
+                    op=ALU.add,
+                )
                 nc.vector.reciprocal(out=inverse[:], in_=total[:])
             nc.vector.tensor_tensor(
                 out=a_tiles[qi][:, heads, :],

@@ -26,14 +26,17 @@ KEY_PASSES = T // K_PASS
 C_PASSES = C // K_PASS
 N_TILES = C // N_TILE
 TILES_PER_PASS = K_PASS // P
-HEADS_PER_GROUP = K_PASS // D
+GROUP = K_PASS // D
 SCALE = 1.0 / math.sqrt(D)
 MASKED = -1.0e30
 
 FLOPS = 2 * 2 * H * (512 * 512 + 512 * 1024) * D + 2 * T * C * C
 
+RAW_BUFS = 3
 E_BUFS = 4
+RESULT_BUFS = 4
 SCALED_BUFS = 4
+GROUPED_BUFS = 4
 CODE_BUFS = 8
 LAG_TRANSPOSE = 2
 LAG_QUANTISE = 3
@@ -67,10 +70,16 @@ def tile_gqa_pb_kernel(tc, q_rot, k_rot, v, Wp, out):
         return 0 <= w < n_works
 
     def ends_group(w):
-        return is_work(w) and (works[w][1] + works[w][2]) % HEADS_PER_GROUP == 0
+        return is_work(w) and (works[w][1] + works[w][2]) % GROUP == 0
 
     def ends_tile(w):
         return is_work(w) and works[w][1] + works[w][2] == H
+
+    def tile_and_group(last):
+        return works[last][0], (works[last][1] + works[last][2]) // GROUP - 1
+
+    def group_works(last):
+        return range(last + 1 - GROUP // works[last][2], last + 1)
 
     with ExitStack() as stack:
         keep = stack.enter_context(tc.tile_pool(name="keep", bufs=1))
@@ -84,17 +93,19 @@ def tile_gqa_pb_kernel(tc, q_rot, k_rot, v, Wp, out):
         k_view = k_rot[0].rearrange("j (n p) d -> n p j d", p=P)
         v_view = v[0].rearrange("j (g u p e) d -> g u p j (e d)", g=KEY_PASSES, u=2, p=P, e=2)
         wp_view = Wp.rearrange("(g u p e) n -> g u p (e n)", g=C_PASSES, u=2, p=P, e=2)
-        q_raw = []
-        k_raw = []
-        for qi in range(Q_TILES):
-            q_raw.append(keep.tile([P, H, D], BF16, name="q_raw%d" % qi))
-            k_raw.append(keep.tile([P, H_KV, D], BF16, name="k_raw%d" % qi))
+        q_raw = {}
+        k_raw = {}
         v_raw = keep.tile([P, KEY_PASSES, H_KV, PACK, D], BF16)
         wp_raw = keep.tile([P, C_PASSES, PACK, C], BF16)
 
         def load_qk(qi):
-            nc.sync.dma_start(out=q_raw[qi][:], in_=q_view[qi])
-            nc.sync.dma_start(out=k_raw[qi][:], in_=k_view[qi])
+            k_tile = ring.tile([P, H_KV, D], BF16, tag="k_raw", bufs=RAW_BUFS)
+            nc.sync.dma_start(out=k_tile[:], in_=k_view[qi])
+            k_raw[qi] = k_tile
+            q_tile = ring.tile([P, H, D], BF16, tag="q_raw", bufs=RAW_BUFS)
+            for heads in (slice(0, H_KV), slice(H_KV, H)):
+                nc.sync.dma_start(out=q_tile[:, heads, :], in_=q_view[qi][:, heads, :])
+            q_raw[qi] = q_tile
 
         def load_v(g):
             for u in range(2):
@@ -118,8 +129,6 @@ def tile_gqa_pb_kernel(tc, q_rot, k_rot, v, Wp, out):
         load_wp(1)
         load_wp(2)
         load_v(1)
-        for qi in range(3, Q_TILES):
-            load_qk(qi)
 
         ident_bf = keep.tile([P, P], BF16)
         make_identity(nc, ident_bf[:])
@@ -147,7 +156,7 @@ def tile_gqa_pb_kernel(tc, q_rot, k_rot, v, Wp, out):
         for block in range(2):
             row = []
             for b in range(E_BUFS):
-                e_tile = keep.tile([P, 2, K_PASS], BF16, name="e%d_%d" % (block, b))
+                e_tile = keep.tile([P, 2 * K_PASS], BF16, name="e%d_%d" % (block, b))
                 nc.vector.memset(e_tile[:], 0.0)
                 row.append(e_tile)
             e_tiles.append(row)
@@ -214,14 +223,15 @@ def tile_gqa_pb_kernel(tc, q_rot, k_rot, v, Wp, out):
             if part == 0:
                 qT_tile = ring.tile([P, H, P], BF16, tag="qT")
                 qT[qi] = qT_tile
+            first = H_KV * (part - 1)
             xt = psum_tr.tile([P, H_KV, P], BF16, tag="tr")
             for i in range(H_KV):
-                src = k_raw[qi][:, i, :] if part == 2 else q_raw[qi][:, H_KV * part + i, :]
+                src = k_raw[qi][:, i, :] if part == 0 else q_raw[qi][:, first + i, :]
                 nc.tensor.transpose(xt[:, i, :], src, ident_bf[:])
-            if part == 2:
+            if part == 0:
                 nc.scalar.copy(out=kT[:, :, P * qi : P * (qi + 1)], in_=xt[:])
             else:
-                nc.scalar.copy(out=qT[qi][:, H_KV * part : H_KV * (part + 1), :], in_=xt[:])
+                nc.scalar.copy(out=qT[qi][:, first : first + H_KV, :], in_=xt[:])
 
         def scores(w):
             qi = works[w][0]
@@ -249,13 +259,12 @@ def tile_gqa_pb_kernel(tc, q_rot, k_rot, v, Wp, out):
             s_banks[w] = banks
 
         def row_max(w):
-            heads_per_work = works[w][2]
-            scaled = ring.tile([P, 2, N_TILE], F32, tag="scaled", bufs=SCALED_BUFS)
+            scaled = ring.tile([P, 2 * N_TILE], F32, tag="scaled", bufs=SCALED_BUFS)
             bias = small.tile([P, 2], F32, tag="bias")
             for c in range(2):
                 n_keys = half_of(w, c)[2]
                 nc.vector.tensor_scalar(
-                    out=scaled[:, c, 0:n_keys],
+                    out=scaled[:, N_TILE * c : N_TILE * c + n_keys],
                     in0=s_banks[w][c][:, 0:n_keys],
                     scalar1=-SCALE,
                     scalar2=None,
@@ -264,41 +273,37 @@ def tile_gqa_pb_kernel(tc, q_rot, k_rot, v, Wp, out):
                     accum_out=bias[:, c : c + 1],
                 )
             scaled_scores[w] = scaled
-            if heads_per_work == 2:
-                neg_max[w] = (bias[:, 0:1], bias[:, 1:2])
-            else:
+            if works[w][2] == 1:
                 joined = small.tile([P, 1], F32, tag="joined")
                 nc.gpsimd.tensor_scalar(
                     out=joined[:], in0=bias[:, 0:1], scalar1=bias[:, 1:2], scalar2=None, op0=ALU.min
                 )
-                neg_max[w] = (joined[:], joined[:])
+                bias = joined
+            neg_max[w] = bias
 
         def exponentials(w):
             qi, first_head, heads_per_work = works[w]
             if first_head == 0:
-                sums = ring.tile([P, H, 2], F32, tag="row_sums")
+                sums = ring.tile([P, H], F32, tag="row_sums")
                 row_sums[qi] = sums
-            for c in range(2):
-                head, key0, n_keys = half_of(w, c)
-                part = 0 if heads_per_work == 2 else c
+            for c in range(heads_per_work):
+                head = first_head + c
+                cols = slice(K_PASS * c, K_PASS * c + P * (qi + 1))
                 nc.scalar.activation(
-                    out=e_of(w)[:, c, 0:n_keys],
-                    in_=scaled_scores[w][:, c, 0:n_keys],
+                    out=e_of(w)[:, cols],
+                    in_=scaled_scores[w][:, cols],
                     func=ACT.Exp,
-                    bias=neg_max[w][c],
+                    bias=neg_max[w][:, c : c + 1],
                     scale=-1.0,
-                    accum_out=row_sums[qi][:, head, part : part + 1],
+                    accum_out=row_sums[qi][:, head : head + 1],
                 )
 
         def transpose_e(w):
             e_words = e_of(w)[:].bitcast(F32)
             xt = psum_tr.tile([P, 4, P], F32, tag="tr")
-            for c in range(2):
-                for u in range(2):
-                    nc.tensor.transpose(
-                        xt[:, 2 * c + u, :], e_words[:, c, P * u : P * (u + 1)], ident_f32[:]
-                    )
-            grouped = ring.tile([P, 2 * K_PASS], BF16, align_bytes=64, tag="e_grouped", bufs=3)
+            for i in range(4):
+                nc.tensor.transpose(xt[:, i, :], e_words[:, P * i : P * (i + 1)], ident_f32[:])
+            grouped = ring.tile([P, 2 * K_PASS], BF16, align_bytes=64, tag="e_grouped", bufs=GROUPED_BUFS)
             nc.scalar.copy(
                 out=grouped[:].bitcast(F32).rearrange("p (c q u) -> p c q u", c=2, u=2),
                 in_=xt[:].rearrange("p (c u) q -> p c q u", u=2),
@@ -316,18 +321,15 @@ def tile_gqa_pb_kernel(tc, q_rot, k_rot, v, Wp, out):
             e_codes[w] = codes
             e_scales[w] = scales
 
-        def group_works(last):
-            return range(last + 1 - HEADS_PER_GROUP // works[last][2], last + 1)
-
         def e_times_v(last):
-            pv = psum_acc.tile([P, HEADS_PER_GROUP, D], F32, tag="acc")
-            for w in group_works(last):
+            pv = psum_acc.tile([P, GROUP, D], F32, tag="acc")
+            for w in reversed(group_works(last)):
                 lone = works[w][2] == 2
                 for c in range(2):
                     head, key0, n_keys = half_of(w, c)
                     g = key0 // K_PASS
                     nc.tensor.matmul_mx(
-                        out=pv[:, head % HEADS_PER_GROUP, :],
+                        out=pv[:, head % GROUP, :],
                         lhsT=e_codes[w][:, c, :].bitcast(FP8X4),
                         lhsT_scale=e_scales[w][:, c, :],
                         rhs=v_codes[:, g, head // 2, :].bitcast(FP8X4),
@@ -338,77 +340,64 @@ def tile_gqa_pb_kernel(tc, q_rot, k_rot, v, Wp, out):
             pv_banks[last] = pv
 
         def normalise(last):
-            qi, first_head, heads_per_work = works[last]
-            group = (first_head + heads_per_work) // HEADS_PER_GROUP - 1
-            heads = slice(HEADS_PER_GROUP * group, HEADS_PER_GROUP * (group + 1))
+            qi, group = tile_and_group(last)
+            heads = slice(GROUP * group, GROUP * (group + 1))
             if group == 0:
                 a_tile = ring.tile([P, H, D], BF16, tag="a")
                 a_tiles[qi] = a_tile
-            inverse = small.tile([P, HEADS_PER_GROUP], F32, tag="inverse")
-            if heads_per_work == 2:
-                nc.vector.reciprocal(out=inverse[:], in_=row_sums[qi][:, heads, 0])
-            else:
-                total = small.tile([P, HEADS_PER_GROUP], F32, tag="total")
-                nc.gpsimd.tensor_tensor(
-                    out=total[:],
-                    in0=row_sums[qi][:, heads, 0],
-                    in1=row_sums[qi][:, heads, 1],
-                    op=ALU.add,
-                )
-                nc.vector.reciprocal(out=inverse[:], in_=total[:])
+            inverse = small.tile([P, GROUP], F32, tag="inverse")
+            nc.vector.reciprocal(out=inverse[:], in_=row_sums[qi][:, heads])
             nc.vector.tensor_tensor(
                 out=a_tiles[qi][:, heads, :],
                 in0=pv_banks[last][:],
-                in1=inverse[:].unsqueeze(2).to_broadcast([P, HEADS_PER_GROUP, D]),
+                in1=inverse[:].unsqueeze(2).to_broadcast([P, GROUP, D]),
                 op=ALU.mult,
             )
 
-        def transpose_a(qi):
+        def transpose_a(last):
+            qi, group = tile_and_group(last)
+            if group == 0:
+                grouped = ring.tile([P, C_PASSES, K_PASS], BF16, align_bytes=64, tag="a_grouped")
+                a_grouped[qi] = grouped
             a_words = a_tiles[qi][:].rearrange("p h d -> p (h d)").bitcast(F32)
-            grouped = ring.tile([P, C_PASSES * K_PASS], BF16, align_bytes=64, tag="a_grouped")
-            for first_pass, n_passes in ((0, 2), (2, 1)):
-                xt = psum_tr.tile([P, 4, P], F32, tag="tr")
-                for i in range(2 * n_passes):
-                    word0 = 2 * P * first_pass + P * i
-                    nc.tensor.transpose(xt[:, i, :], a_words[:, word0 : word0 + P], ident_f32[:])
-                nc.vector.tensor_copy(
-                    out=grouped[:, K_PASS * first_pass : K_PASS * (first_pass + n_passes)]
-                    .bitcast(F32)
-                    .rearrange("p (c q u) -> p c q u", c=n_passes, u=2),
-                    in_=xt[:, 0 : 2 * n_passes, :].rearrange("p (c u) q -> p c q u", u=2),
-                )
-            a_grouped[qi] = grouped
+            xt = psum_tr.tile([P, 2, P], F32, tag="tr")
+            for u in range(2):
+                word0 = P * (2 * group + u)
+                nc.tensor.transpose(xt[:, u, :], a_words[:, word0 : word0 + P], ident_f32[:])
+            nc.vector.tensor_copy(
+                out=a_grouped[qi][:, group, :].bitcast(F32).rearrange("p (q u) -> p q u", u=2),
+                in_=xt[:].rearrange("p u q -> p q u"),
+            )
 
-        def quantise_a(qi):
-            codes = ring.tile([P, C_PASSES, P], U32, align_bytes=64, tag="a_codes")
-            scales = ring.tile([P, C_PASSES, P], U8, align_bytes=64, tag="a_scales")
-            for first_pass, n_passes in ((0, 2), (2, 1)):
-                passes = slice(first_pass, first_pass + n_passes)
-                nc.vector.quantize_mx(
-                    out=codes[:, passes, :].rearrange("p c q -> p (c q)").bitcast(FP8X4),
-                    scales=scales[:, passes, :].rearrange("p c q -> p (c q)"),
-                    in_=a_grouped[qi][:, K_PASS * first_pass : K_PASS * (first_pass + n_passes)],
-                )
-            a_codes[qi] = codes
-            a_scales[qi] = scales
+        def quantise_a(last):
+            qi, group = tile_and_group(last)
+            if group == 0:
+                codes = ring.tile([P, C_PASSES, P], U32, align_bytes=64, tag="a_codes")
+                scales = ring.tile([P, C_PASSES, P], U8, align_bytes=64, tag="a_scales")
+                a_codes[qi] = codes
+                a_scales[qi] = scales
+            nc.vector.quantize_mx(
+                out=a_codes[qi][:, group, :].bitcast(FP8X4),
+                scales=a_scales[qi][:, group, :],
+                in_=a_grouped[qi][:, group, :],
+            )
 
-        def project(qi):
-            result = ring.tile([P, C], F32, tag="result")
-            for nt in range(N_TILES):
-                cols = slice(N_TILE * nt, N_TILE * (nt + 1))
-                acc = psum_acc.tile([P, N_TILE], F32, tag="acc")
-                for g in range(C_PASSES):
-                    nc.tensor.matmul_mx(
-                        out=acc[:],
-                        lhsT=a_codes[qi][:, g, :].bitcast(FP8X4),
-                        lhsT_scale=a_scales[qi][:, g, :],
-                        rhs=wp_codes[:, g, cols].bitcast(FP8X4),
-                        rhs_scale=wp_scales[:, g, cols],
-                        start=(g == 0),
-                        stop=(g == C_PASSES - 1),
-                    )
-                nc.scalar.copy(out=result[:, cols], in_=acc[:])
-                nc.sync.dma_start(out=out[0, P * qi : P * (qi + 1), cols], in_=result[:, cols])
+        def project(qi, nt):
+            cols = slice(N_TILE * nt, N_TILE * (nt + 1))
+            acc = psum_acc.tile([P, N_TILE], F32, tag="acc")
+            for g in range(C_PASSES):
+                nc.tensor.matmul_mx(
+                    out=acc[:],
+                    lhsT=a_codes[qi][:, g, :].bitcast(FP8X4),
+                    lhsT_scale=a_scales[qi][:, g, :],
+                    rhs=wp_codes[:, g, cols].bitcast(FP8X4),
+                    rhs_scale=wp_scales[:, g, cols],
+                    start=(g == 0),
+                    stop=(g == C_PASSES - 1),
+                )
+            result = ring.tile([P, N_TILE], F32, tag="result", bufs=RESULT_BUFS)
+            nc.scalar.copy(out=result[:], in_=acc[:])
+            nc.sync.dma_start(out=out[0, P * qi : P * (qi + 1), cols], in_=result[:])
 
         for part in range(3):
             transpose_qk(0, part)
@@ -416,11 +405,13 @@ def tile_gqa_pb_kernel(tc, q_rot, k_rot, v, Wp, out):
             prepare_v(0, pair)
 
         first_work_of_tile = 0
-        for w in range(n_works + LAG_PROJECT + 1):
+        for w in range(n_works + LAG_PROJECT + N_TILES):
             if is_work(w):
                 qi = works[w][0]
                 if works[w][1] == 0:
                     first_work_of_tile = w
+                    if qi + RAW_BUFS < Q_TILES:
+                        load_qk(qi + RAW_BUFS)
                 scores(w)
             if is_work(w - LAG_QUANTISE):
                 quantise_e(w - LAG_QUANTISE)
@@ -443,9 +434,10 @@ def tile_gqa_pb_kernel(tc, q_rot, k_rot, v, Wp, out):
                 e_times_v(w - LAG_PV)
             if ends_group(w - LAG_NORMALISE):
                 normalise(w - LAG_NORMALISE)
-            if ends_tile(w - LAG_A_TRANSPOSE):
-                transpose_a(works[w - LAG_A_TRANSPOSE][0])
-            if ends_tile(w - LAG_A_QUANTISE):
-                quantise_a(works[w - LAG_A_QUANTISE][0])
-            if ends_tile(w - LAG_PROJECT):
-                project(works[w - LAG_PROJECT][0])
+            if ends_group(w - LAG_A_TRANSPOSE):
+                transpose_a(w - LAG_A_TRANSPOSE)
+            if ends_group(w - LAG_A_QUANTISE):
+                quantise_a(w - LAG_A_QUANTISE)
+            for nt in range(N_TILES):
+                if ends_tile(w - LAG_PROJECT - nt):
+                    project(works[w - LAG_PROJECT - nt][0], nt)

@@ -66,6 +66,9 @@ def tile_gqa_pb_kernel(tc, q_rot, k_rot, v, Wp, out):
             return first_head + c, 0, n_keys
         return first_head, K_PASS * c, (K_PASS if c == 0 else n_keys - K_PASS)
 
+    def is_short(qi):
+        return qi < TILES_PER_PASS
+
     def is_work(w):
         return 0 <= w < n_works
 
@@ -202,7 +205,8 @@ def tile_gqa_pb_kernel(tc, q_rot, k_rot, v, Wp, out):
         def regroup_wp(chunk):
             g, nt = divmod(chunk, N_TILES)
             grouped = ring.tile([P, N_TILE, PACK], BF16, align_bytes=64, tag="wp_grouped")
-            nc.vector.tensor_copy(
+            regroup = nc.scalar.copy if nt == 0 else nc.vector.tensor_copy
+            regroup(
                 out=grouped[:].rearrange("p (c i) t -> p c t i", i=4),
                 in_=wp_raw[:, g, :, N_TILE * nt : N_TILE * (nt + 1)].rearrange(
                     "p t (c i) -> p c t i", i=4
@@ -364,7 +368,8 @@ def tile_gqa_pb_kernel(tc, q_rot, k_rot, v, Wp, out):
             for u in range(2):
                 word0 = P * (2 * group + u)
                 nc.tensor.transpose(xt[:, u, :], a_words[:, word0 : word0 + P], ident_f32[:])
-            nc.vector.tensor_copy(
+            copy_out = nc.scalar.copy if is_short(qi) else nc.vector.tensor_copy
+            copy_out(
                 out=a_grouped[qi][:, group, :].bitcast(F32).rearrange("p (q u) -> p q u", u=2),
                 in_=xt[:].rearrange("p u q -> p q u"),
             )
@@ -396,7 +401,8 @@ def tile_gqa_pb_kernel(tc, q_rot, k_rot, v, Wp, out):
                     stop=(g == C_PASSES - 1),
                 )
             result = ring.tile([P, N_TILE], F32, tag="result", bufs=RESULT_BUFS)
-            nc.scalar.copy(out=result[:], in_=acc[:])
+            copy_out = nc.vector.tensor_copy if nt == 1 and not is_short(qi) else nc.scalar.copy
+            copy_out(out=result[:], in_=acc[:])
             nc.sync.dma_start(out=out[0, P * qi : P * (qi + 1), cols], in_=result[:])
 
         for part in range(3):

@@ -33,11 +33,11 @@ MASKED = -1.0e30
 FLOPS = 2 * 2 * H * (512 * 512 + 512 * 1024) * D + 2 * T * C * C
 
 RAW_BUFS = 3
-E_BUFS = 4
+E_BUFS = 6
 RESULT_BUFS = 4
-SCALED_BUFS = 4
+SCALED_BUFS = 6
 GROUPED_BUFS = 4
-CODE_BUFS = 8
+CODE_BUFS = 12
 LAG_TRANSPOSE = 2
 LAG_QUANTISE = 3
 LAG_PV = 4
@@ -88,8 +88,8 @@ def tile_gqa_pb_kernel(tc, q_rot, k_rot, v, Wp, out):
         keep = stack.enter_context(tc.tile_pool(name="keep", bufs=1))
         ring = stack.enter_context(tc.tile_pool(name="ring", bufs=2))
         small = stack.enter_context(tc.tile_pool(name="small", bufs=4))
-        psum_s = stack.enter_context(tc.psum_pool(name="psum_s", bufs=3))
-        psum_tr = stack.enter_context(tc.psum_pool(name="psum_tr", bufs=3))
+        psum_s = stack.enter_context(tc.psum_pool(name="psum_s", bufs=4))
+        psum_tr = stack.enter_context(tc.psum_pool(name="psum_tr", bufs=2))
         psum_acc = stack.enter_context(tc.psum_pool(name="psum_acc", bufs=2))
 
         q_view = q_rot[0].rearrange("h (n p) d -> n p h d", p=P)
@@ -135,21 +135,19 @@ def tile_gqa_pb_kernel(tc, q_rot, k_rot, v, Wp, out):
 
         ident_bf = keep.tile([P, P], BF16)
         make_identity(nc, ident_bf[:])
-        ident_f32 = keep.tile([P, P], F32)
-        make_identity(nc, ident_f32[:])
-        mask_f32 = keep.tile([P, P], F32)
-        nc.gpsimd.memset(mask_f32[:], 0.0)
+        mask_bf = keep.tile([P, P], BF16)
+        nc.gpsimd.memset(mask_bf[:], 0.0)
         nc.gpsimd.affine_select(
-            out=mask_f32[:],
-            in_=mask_f32[:],
+            out=mask_bf[:],
+            in_=mask_bf[:],
             compare_op=ALU.is_ge,
             fill=MASKED,
             base=0,
             pattern=[[-1, P]],
             channel_multiplier=1,
         )
-        mask_bf = keep.tile([P, P], BF16)
-        nc.vector.tensor_copy(out=mask_bf[:], in_=mask_f32[:])
+        ident_f32 = keep.tile([P, P], F32)
+        make_identity(nc, ident_f32[:])
         warm_in = keep.tile([P, 1], F32)
         warm_out = keep.tile([P, 1], F32)
         nc.vector.memset(warm_in[:], 0.0)
@@ -159,8 +157,8 @@ def tile_gqa_pb_kernel(tc, q_rot, k_rot, v, Wp, out):
         for block in range(2):
             row = []
             for b in range(E_BUFS):
-                e_tile = keep.tile([P, 2 * K_PASS], BF16, name="e%d_%d" % (block, b))
-                nc.vector.memset(e_tile[:], 0.0)
+                e_tile = keep.tile([P, 2 * K_PASS], BF16, align_bytes=64, name="e%d_%d" % (block, b))
+                nc.gpsimd.memset(e_tile[:].bitcast(U32), 0)
                 row.append(e_tile)
             e_tiles.append(row)
 
@@ -187,6 +185,11 @@ def tile_gqa_pb_kernel(tc, q_rot, k_rot, v, Wp, out):
         a_codes = {}
         a_scales = {}
         wp_grouped = {}
+        e_transposed = {}
+        a_transposed = {}
+        qk_transposed = {}
+        projected = {}
+        last_banks = []
 
         def prepare_v(g, pair):
             grouped = ring.tile([P, 2, D, PACK], BF16, align_bytes=64, tag="v_grouped")
@@ -232,15 +235,20 @@ def tile_gqa_pb_kernel(tc, q_rot, k_rot, v, Wp, out):
             for i in range(H_KV):
                 src = k_raw[qi][:, i, :] if part == 0 else q_raw[qi][:, first + i, :]
                 nc.tensor.transpose(xt[:, i, :], src, ident_bf[:])
-            if part == 0:
-                nc.scalar.copy(out=kT[:, :, P * qi : P * (qi + 1)], in_=xt[:])
-            else:
-                nc.scalar.copy(out=qT[qi][:, first : first + H_KV, :], in_=xt[:])
+            qk_transposed[qi, part] = xt
 
-        def scores(w):
+        def copy_qk(qi, part):
+            first = H_KV * (part - 1)
+            xt = qk_transposed[qi, part]
+            copy_out = nc.vector.tensor_copy if qi == 0 and part != 1 else nc.scalar.copy
+            if part == 0:
+                copy_out(out=kT[:, :, P * qi : P * (qi + 1)], in_=xt[:])
+            else:
+                copy_out(out=qT[qi][:, first : first + H_KV, :], in_=xt[:])
+
+        def scores(w, c):
             qi = works[w][0]
-            banks = []
-            for c in range(2):
+            if True:
                 head, key0, n_keys = half_of(w, c)
                 s = psum_s.tile([P, N_TILE], F32, tag="s")
                 on_diagonal = key0 + n_keys == P * (qi + 1)
@@ -259,31 +267,27 @@ def tile_gqa_pb_kernel(tc, q_rot, k_rot, v, Wp, out):
                         start=False,
                         stop=True,
                     )
-                banks.append(s)
-            s_banks[w] = banks
+                s_banks[w, c] = s
 
-        def row_max(w):
-            scaled = ring.tile([P, 2 * N_TILE], F32, tag="scaled", bufs=SCALED_BUFS)
-            bias = small.tile([P, 2], F32, tag="bias")
-            for c in range(2):
+        def row_max(w, c):
+            if c == 0:
+                scaled = ring.tile([P, 2 * N_TILE], F32, tag="scaled", bufs=SCALED_BUFS)
+                bias = small.tile([P, 2], F32, tag="bias", bufs=SCALED_BUFS)
+                scaled_scores[w] = scaled
+                neg_max[w] = bias
+            scaled = scaled_scores[w]
+            bias = neg_max[w]
+            if True:
                 n_keys = half_of(w, c)[2]
                 nc.vector.tensor_scalar(
                     out=scaled[:, N_TILE * c : N_TILE * c + n_keys],
-                    in0=s_banks[w][c][:, 0:n_keys],
+                    in0=s_banks[w, c][:, 0:n_keys],
                     scalar1=-SCALE,
-                    scalar2=None,
+                    scalar2=bias[:, 0:1] if works[w][2] == 1 and c == 1 else None,
                     op0=ALU.mult,
                     op1=ALU.min,
                     accum_out=bias[:, c : c + 1],
                 )
-            scaled_scores[w] = scaled
-            if works[w][2] == 1:
-                joined = small.tile([P, 1], F32, tag="joined")
-                nc.gpsimd.tensor_scalar(
-                    out=joined[:], in0=bias[:, 0:1], scalar1=bias[:, 1:2], scalar2=None, op0=ALU.min
-                )
-                bias = joined
-            neg_max[w] = bias
 
         def exponentials(w):
             qi, first_head, heads_per_work = works[w]
@@ -297,7 +301,7 @@ def tile_gqa_pb_kernel(tc, q_rot, k_rot, v, Wp, out):
                     out=e_of(w)[:, cols],
                     in_=scaled_scores[w][:, cols],
                     func=ACT.Exp,
-                    bias=neg_max[w][:, c : c + 1],
+                    bias=neg_max[w][:, 1:2] if heads_per_work == 1 else neg_max[w][:, c : c + 1],
                     scale=-1.0,
                     accum_out=row_sums[qi][:, head : head + 1],
                 )
@@ -307,6 +311,10 @@ def tile_gqa_pb_kernel(tc, q_rot, k_rot, v, Wp, out):
             xt = psum_tr.tile([P, 4, P], F32, tag="tr")
             for i in range(4):
                 nc.tensor.transpose(xt[:, i, :], e_words[:, P * i : P * (i + 1)], ident_f32[:])
+            e_transposed[w] = xt
+
+        def regroup_e(w):
+            xt = e_transposed[w]
             grouped = ring.tile([P, 2 * K_PASS], BF16, align_bytes=64, tag="e_grouped", bufs=GROUPED_BUFS)
             nc.scalar.copy(
                 out=grouped[:].bitcast(F32).rearrange("p (c q u) -> p c q u", c=2, u=2),
@@ -368,6 +376,11 @@ def tile_gqa_pb_kernel(tc, q_rot, k_rot, v, Wp, out):
             for u in range(2):
                 word0 = P * (2 * group + u)
                 nc.tensor.transpose(xt[:, u, :], a_words[:, word0 : word0 + P], ident_f32[:])
+            a_transposed[last] = xt
+
+        def regroup_a(last):
+            qi, group = tile_and_group(last)
+            xt = a_transposed[last]
             copy_out = nc.scalar.copy if is_short(qi) else nc.vector.tensor_copy
             copy_out(
                 out=a_grouped[qi][:, group, :].bitcast(F32).rearrange("p (q u) -> p q u", u=2),
@@ -400,50 +413,94 @@ def tile_gqa_pb_kernel(tc, q_rot, k_rot, v, Wp, out):
                     start=(g == 0),
                     stop=(g == C_PASSES - 1),
                 )
+            projected[qi, nt] = acc
+
+        def store_result(qi, nt):
+            acc = projected[qi, nt]
+            cols = slice(N_TILE * nt, N_TILE * (nt + 1))
             result = ring.tile([P, N_TILE], F32, tag="result", bufs=RESULT_BUFS)
             copy_out = nc.vector.tensor_copy if nt == 1 and not is_short(qi) else nc.scalar.copy
             copy_out(out=result[:], in_=acc[:])
             nc.sync.dma_start(out=out[0, P * qi : P * (qi + 1), cols], in_=result[:])
 
-        for part in range(3):
-            transpose_qk(0, part)
-        for pair in range(H_KV // 2):
-            prepare_v(0, pair)
-
-        first_work_of_tile = 0
-        for w in range(n_works + LAG_PROJECT + N_TILES):
-            if is_work(w):
-                qi = works[w][0]
-                if works[w][1] == 0:
-                    first_work_of_tile = w
-                    if qi + RAW_BUFS < Q_TILES:
-                        load_qk(qi + RAW_BUFS)
-                scores(w)
-            if is_work(w - LAG_QUANTISE):
-                quantise_e(w - LAG_QUANTISE)
-            if is_work(w):
-                row_max(w)
-            if is_work(w - LAG_TRANSPOSE):
-                transpose_e(w - LAG_TRANSPOSE)
-            if is_work(w):
-                part = w - first_work_of_tile
-                if part < 3 and qi + 1 < Q_TILES:
-                    transpose_qk(qi + 1, part)
-                exponentials(w)
-            if w < WP_CHUNKS:
-                regroup_wp(w)
-            if 1 <= w <= WP_CHUNKS:
-                quantise_wp(w - 1)
-            if 0 <= w - V_LATE_START < H_KV // 2:
-                prepare_v(1, w - V_LATE_START)
-            if ends_group(w - LAG_PV):
-                e_times_v(w - LAG_PV)
-            if ends_group(w - LAG_NORMALISE):
-                normalise(w - LAG_NORMALISE)
-            if ends_group(w - LAG_A_TRANSPOSE):
-                transpose_a(w - LAG_A_TRANSPOSE)
-            if ends_group(w - LAG_A_QUANTISE):
-                quantise_a(w - LAG_A_QUANTISE)
+        def project_last_tile(g):
+            qi = Q_TILES - 1
             for nt in range(N_TILES):
-                if ends_tile(w - LAG_PROJECT - nt):
-                    project(works[w - LAG_PROJECT - nt][0], nt)
+                if g == 0:
+                    bank = psum_s.tile([P, N_TILE], F32, tag="s")
+                    last_banks.append(bank)
+                cols = slice(N_TILE * nt, N_TILE * (nt + 1))
+                nc.tensor.matmul_mx(
+                    out=last_banks[nt][:],
+                    lhsT=a_codes[qi][:, g, :].bitcast(FP8X4),
+                    lhsT_scale=a_scales[qi][:, g, :],
+                    rhs=wp_codes[:, g, cols].bitcast(FP8X4),
+                    rhs_scale=wp_scales[:, g, cols],
+                    start=(g == 0),
+                    stop=(g == C_PASSES - 1),
+                )
+                projected[qi, nt] = last_banks[nt]
+
+
+        LE, LM, LT, LC, LQ, LPV = 2, 1, 4, 4, 5, 6
+        LN, LAT, LAQ, LP = LPV + 1, LPV + 3, LPV + 4, LPV + 5
+        LAC, QK0, QKC, RC = LPV + 3, 2, 0, 0
+        WP0, V1, V0, WPS = 4, 14, 1, 1
+        with tc.manual_schedule():
+            for part in range(3):
+                transpose_qk(0, part)
+                copy_qk(0, part)
+            for w in range(n_works + LP + N_TILES):
+                if is_work(w) and works[w][1] == 0 and works[w][0] + RAW_BUFS < Q_TILES:
+                    load_qk(works[w][0] + RAW_BUFS)
+                if is_work(w - LT):
+                    transpose_e(w - LT)
+                if ends_group(w - LAT):
+                    transpose_a(w - LAT)
+                if is_work(w - QK0) and works[w - QK0][1] // works[w - QK0][2] < 3 and works[w - QK0][0] + 1 < Q_TILES:
+                    transpose_qk(works[w - QK0][0] + 1, works[w - QK0][1] // works[w - QK0][2])
+                if is_work(w):
+                    scores(w, 0)
+                if ends_group(w - LPV):
+                    e_times_v(w - LPV)
+                for nt in range(N_TILES):
+                    if ends_tile(w - LP - nt) and works[w - LP - nt][0] < Q_TILES - 1:
+                        project(works[w - LP - nt][0], nt)
+                last = w - LAQ - 1
+                if is_work(last) and ends_group(last) and works[last][0] == Q_TILES - 1:
+                    project_last_tile(tile_and_group(last)[1])
+                if is_work(w):
+                    scores(w, 1)
+                if is_work(w - LM):
+                    row_max(w - LM, 0)
+                if ends_group(w - LN):
+                    normalise(w - LN)
+                if is_work(w - LQ):
+                    quantise_e(w - LQ)
+                if is_work(w - LM):
+                    row_max(w - LM, 1)
+                if ends_group(w - LAQ):
+                    quantise_a(w - LAQ)
+                if is_work(w - LC):
+                    regroup_e(w - LC)
+                if ends_group(w - LAC):
+                    regroup_a(w - LAC)
+                if is_work(w - QK0 - QKC) and works[w - QK0 - QKC][1] // works[w - QK0 - QKC][2] < 3 and works[w - QK0 - QKC][0] + 1 < Q_TILES:
+                    copy_qk(works[w - QK0 - QKC][0] + 1, works[w - QK0 - QKC][1] // works[w - QK0 - QKC][2])
+                if is_work(w - LE):
+                    exponentials(w - LE)
+                if (w - WP0) % WPS == 0 and 0 <= (w - WP0) // WPS < WP_CHUNKS:
+                    regroup_wp((w - WP0) // WPS)
+                if (w - WP0 - 1) % WPS == 0 and 0 <= (w - WP0 - 1) // WPS < WP_CHUNKS:
+                    quantise_wp((w - WP0 - 1) // WPS)
+                if V1 <= w < V1 + H_KV // 2:
+                    prepare_v(1, w - V1)
+                if V0 <= w < V0 + H_KV // 2:
+                    prepare_v(0, w - V0)
+                for nt in range(N_TILES):
+                    if ends_tile(w - LP - RC - nt) and works[w - LP - RC - nt][0] < Q_TILES - 1:
+                        store_result(works[w - LP - RC - nt][0], nt)
+                last = w - LAQ - 1
+                if is_work(last) and ends_tile(last) and works[last][0] == Q_TILES - 1:
+                    for nt in range(N_TILES):
+                        store_result(Q_TILES - 1, nt)

@@ -88,8 +88,8 @@ def tile_gqa_pb_kernel(tc, q_rot, k_rot, v, Wp, out):
         keep = stack.enter_context(tc.tile_pool(name="keep", bufs=1))
         ring = stack.enter_context(tc.tile_pool(name="ring", bufs=2))
         small = stack.enter_context(tc.tile_pool(name="small", bufs=4))
-        psum_s = stack.enter_context(tc.psum_pool(name="psum_s", bufs=4))
-        psum_tr = stack.enter_context(tc.psum_pool(name="psum_tr", bufs=2))
+        psum_s = stack.enter_context(tc.psum_pool(name="psum_s", bufs=3))
+        psum_tr = stack.enter_context(tc.psum_pool(name="psum_tr", bufs=3))
         psum_acc = stack.enter_context(tc.psum_pool(name="psum_acc", bufs=2))
 
         q_view = q_rot[0].rearrange("h (n p) d -> n p h d", p=P)
@@ -158,7 +158,11 @@ def tile_gqa_pb_kernel(tc, q_rot, k_rot, v, Wp, out):
             row = []
             for b in range(E_BUFS):
                 e_tile = keep.tile([P, 2 * K_PASS], BF16, align_bytes=64, name="e%d_%d" % (block, b))
-                nc.gpsimd.memset(e_tile[:].bitcast(U32), 0)
+                words = e_tile[:].rearrange("p (c k) -> p c k", c=2).bitcast(U32)
+                if block == 0:
+                    nc.gpsimd.memset(words[:, :, P // 2 :], 0)
+                else:
+                    nc.gpsimd.memset(words[:, 1:2, P // 2 :], 0)
                 row.append(e_tile)
             e_tiles.append(row)
 
@@ -185,6 +189,7 @@ def tile_gqa_pb_kernel(tc, q_rot, k_rot, v, Wp, out):
         a_codes = {}
         a_scales = {}
         wp_grouped = {}
+        inverses = {}
         e_transposed = {}
         a_transposed = {}
         qk_transposed = {}
@@ -292,7 +297,7 @@ def tile_gqa_pb_kernel(tc, q_rot, k_rot, v, Wp, out):
         def exponentials(w):
             qi, first_head, heads_per_work = works[w]
             if first_head == 0:
-                sums = ring.tile([P, H], F32, tag="row_sums")
+                sums = ring.tile([P, H], F32, tag="row_sums", bufs=3)
                 row_sums[qi] = sums
             for c in range(heads_per_work):
                 head = first_head + c
@@ -351,14 +356,20 @@ def tile_gqa_pb_kernel(tc, q_rot, k_rot, v, Wp, out):
                     )
             pv_banks[last] = pv
 
+        def invert_sums(last):
+            qi, group = tile_and_group(last)
+            heads = slice(GROUP * group, GROUP * (group + 1))
+            inverse = small.tile([P, GROUP], F32, tag="inverse")
+            nc.vector.reciprocal(out=inverse[:], in_=row_sums[qi][:, heads])
+            inverses[last] = inverse
+
         def normalise(last):
             qi, group = tile_and_group(last)
             heads = slice(GROUP * group, GROUP * (group + 1))
             if group == 0:
                 a_tile = ring.tile([P, H, D], BF16, tag="a")
                 a_tiles[qi] = a_tile
-            inverse = small.tile([P, GROUP], F32, tag="inverse")
-            nc.vector.reciprocal(out=inverse[:], in_=row_sums[qi][:, heads])
+            inverse = inverses[last]
             nc.vector.tensor_tensor(
                 out=a_tiles[qi][:, heads, :],
                 in0=pv_banks[last][:],
@@ -390,8 +401,8 @@ def tile_gqa_pb_kernel(tc, q_rot, k_rot, v, Wp, out):
         def quantise_a(last):
             qi, group = tile_and_group(last)
             if group == 0:
-                codes = ring.tile([P, C_PASSES, P], U32, align_bytes=64, tag="a_codes")
-                scales = ring.tile([P, C_PASSES, P], U8, align_bytes=64, tag="a_scales")
+                codes = ring.tile([P, C_PASSES, P], U32, align_bytes=64, tag="a_codes", bufs=4)
+                scales = ring.tile([P, C_PASSES, P], U8, align_bytes=64, tag="a_scales", bufs=4)
                 a_codes[qi] = codes
                 a_scales[qi] = scales
             nc.vector.quantize_mx(
@@ -442,10 +453,17 @@ def tile_gqa_pb_kernel(tc, q_rot, k_rot, v, Wp, out):
                 projected[qi, nt] = last_banks[nt]
 
 
-        LE, LM, LT, LC, LQ, LPV = 2, 1, 4, 4, 5, 6
+        LE, LM, LT, LC, LQ, LPV = 2, 1, 4, 4, 6, 7
         LN, LAT, LAQ, LP = LPV + 1, LPV + 3, LPV + 4, LPV + 5
         LAC, QK0, QKC, RC = LPV + 3, 2, 0, 0
-        WP0, V1, V0, WPS = 4, 14, 1, 1
+        WPQ = 1
+        WP0, V1, V0, WPS = 6, 19, 1, 1
+        project_at = {}
+        for last in range(n_works):
+            if ends_tile(last) and works[last][0] < Q_TILES - 1:
+                for nt in range(N_TILES):
+                    step = max(last + LP, 16 + N_TILES * works[last][0]) + nt
+                    project_at.setdefault(step, []).append((works[last][0], nt))
         with tc.manual_schedule():
             for part in range(3):
                 transpose_qk(0, part)
@@ -463,9 +481,8 @@ def tile_gqa_pb_kernel(tc, q_rot, k_rot, v, Wp, out):
                     scores(w, 0)
                 if ends_group(w - LPV):
                     e_times_v(w - LPV)
-                for nt in range(N_TILES):
-                    if ends_tile(w - LP - nt) and works[w - LP - nt][0] < Q_TILES - 1:
-                        project(works[w - LP - nt][0], nt)
+                for qi_p, nt in project_at.get(w, []):
+                    project(qi_p, nt)
                 last = w - LAQ - 1
                 if is_work(last) and ends_group(last) and works[last][0] == Q_TILES - 1:
                     project_last_tile(tile_and_group(last)[1])
@@ -473,6 +490,8 @@ def tile_gqa_pb_kernel(tc, q_rot, k_rot, v, Wp, out):
                     scores(w, 1)
                 if is_work(w - LM):
                     row_max(w - LM, 0)
+                if ends_group(w - LPV):
+                    invert_sums(w - LPV)
                 if ends_group(w - LN):
                     normalise(w - LN)
                 if is_work(w - LQ):
@@ -491,15 +510,14 @@ def tile_gqa_pb_kernel(tc, q_rot, k_rot, v, Wp, out):
                     exponentials(w - LE)
                 if (w - WP0) % WPS == 0 and 0 <= (w - WP0) // WPS < WP_CHUNKS:
                     regroup_wp((w - WP0) // WPS)
-                if (w - WP0 - 1) % WPS == 0 and 0 <= (w - WP0 - 1) // WPS < WP_CHUNKS:
-                    quantise_wp((w - WP0 - 1) // WPS)
+                if (w - WP0 - WPQ) % WPS == 0 and 0 <= (w - WP0 - WPQ) // WPS < WP_CHUNKS:
+                    quantise_wp((w - WP0 - WPQ) // WPS)
                 if V1 <= w < V1 + H_KV // 2:
                     prepare_v(1, w - V1)
                 if V0 <= w < V0 + H_KV // 2:
                     prepare_v(0, w - V0)
-                for nt in range(N_TILES):
-                    if ends_tile(w - LP - RC - nt) and works[w - LP - RC - nt][0] < Q_TILES - 1:
-                        store_result(works[w - LP - RC - nt][0], nt)
+                for qi_p, nt in project_at.get(w - RC, []):
+                    store_result(qi_p, nt)
                 last = w - LAQ - 1
                 if is_work(last) and ends_tile(last) and works[last][0] == Q_TILES - 1:
                     for nt in range(N_TILES):

@@ -38,15 +38,22 @@ RESULT_BUFS = 4
 SCALED_BUFS = 6
 GROUPED_BUFS = 4
 CODE_BUFS = 12
-LAG_TRANSPOSE = 2
-LAG_QUANTISE = 3
-LAG_PV = 4
-LAG_NORMALISE = 5
-LAG_A_TRANSPOSE = 6
-LAG_A_QUANTISE = 7
-LAG_PROJECT = 8
+LAG_ROW_MAX = 1
+LAG_EXP = 2
+LAG_TRANSPOSE = 4
+LAG_QUANTISE = 6
+LAG_PV = 7
+LAG_NORMALISE = 8
+LAG_A_TRANSPOSE = 10
+LAG_A_QUANTISE = 11
+LAG_PROJECT = 12
+QK_START = 2
+Q2_STEP = 1
+DRAIN = 2
 WP_CHUNKS = C_PASSES * N_TILES
-V_LATE_START = WP_CHUNKS + 1
+WP_STEPS = [6, 7, 8, 10, 11, 12, 14, 15, 16]
+V_STEPS = [[4, 5, 6], [19, 20, 21]]
+WP_READY = WP_STEPS[-1] + 2
 
 
 def tile_gqa_pb_kernel(tc, q_rot, k_rot, v, Wp, out):
@@ -84,6 +91,17 @@ def tile_gqa_pb_kernel(tc, q_rot, k_rot, v, Wp, out):
     def group_works(last):
         return range(last + 1 - GROUP // works[last][2], last + 1)
 
+    jobs = {}
+    for w in range(n_works):
+        if ends_group(w):
+            jobs[w] = list(group_works(w))
+    jobs[n_works - 2] = jobs[n_works - 1][:-1]
+    jobs[n_works - 1] = jobs[n_works - 1][-1:]
+
+    def job_heads(last):
+        first = works[jobs[last][0]][1]
+        return range(first, works[last][1] + works[last][2])
+
     with ExitStack() as stack:
         keep = stack.enter_context(tc.tile_pool(name="keep", bufs=1))
         ring = stack.enter_context(tc.tile_pool(name="ring", bufs=2))
@@ -101,14 +119,18 @@ def tile_gqa_pb_kernel(tc, q_rot, k_rot, v, Wp, out):
         v_raw = keep.tile([P, KEY_PASSES, H_KV, PACK, D], BF16)
         wp_raw = keep.tile([P, C_PASSES, PACK, C], BF16)
 
-        def load_qk(qi):
+        def load_q_half(qi, half):
+            heads = slice(H_KV * half, H_KV * (half + 1))
+            nc.sync.dma_start(out=q_raw[qi][:, heads, :], in_=q_view[qi][:, heads, :])
+
+        def load_qk(qi, halves=(0, 1)):
             k_tile = ring.tile([P, H_KV, D], BF16, tag="k_raw", bufs=RAW_BUFS)
             nc.sync.dma_start(out=k_tile[:], in_=k_view[qi])
             k_raw[qi] = k_tile
             q_tile = ring.tile([P, H, D], BF16, tag="q_raw", bufs=RAW_BUFS)
-            for heads in (slice(0, H_KV), slice(H_KV, H)):
-                nc.sync.dma_start(out=q_tile[:, heads, :], in_=q_view[qi][:, heads, :])
             q_raw[qi] = q_tile
+            for half in halves:
+                load_q_half(qi, half)
 
         def load_v(g):
             for u in range(2):
@@ -124,9 +146,10 @@ def tile_gqa_pb_kernel(tc, q_rot, k_rot, v, Wp, out):
                     in_=wp_view[g, u],
                 )
 
-        load_qk(0)
-        load_v(0)
+        load_qk(0, (0,))
+        load_q_half(0, 1)
         load_qk(1)
+        load_v(0)
         load_wp(0)
         load_qk(2)
         load_wp(1)
@@ -189,6 +212,7 @@ def tile_gqa_pb_kernel(tc, q_rot, k_rot, v, Wp, out):
         a_codes = {}
         a_scales = {}
         wp_grouped = {}
+        v_grouped = {}
         inverses = {}
         e_transposed = {}
         a_transposed = {}
@@ -203,6 +227,10 @@ def tile_gqa_pb_kernel(tc, q_rot, k_rot, v, Wp, out):
                     out=grouped[:, i, :, :],
                     in_=v_raw[:, g, 2 * pair + i, :, :].rearrange("p t d -> p d t"),
                 )
+            v_grouped[g, pair] = grouped
+
+        def quantise_v(g, pair):
+            grouped = v_grouped[g, pair]
             heads = slice(2 * pair, 2 * pair + 2)
             nc.vector.quantize_mx(
                 out=v_codes[:, g, heads, :].rearrange("p j d -> p (j d)").bitcast(FP8X4),
@@ -213,7 +241,7 @@ def tile_gqa_pb_kernel(tc, q_rot, k_rot, v, Wp, out):
         def regroup_wp(chunk):
             g, nt = divmod(chunk, N_TILES)
             grouped = ring.tile([P, N_TILE, PACK], BF16, align_bytes=64, tag="wp_grouped")
-            regroup = nc.scalar.copy if nt == 0 else nc.vector.tensor_copy
+            regroup = nc.scalar.copy if nt != 1 else nc.vector.tensor_copy
             regroup(
                 out=grouped[:].rearrange("p (c i) t -> p c t i", i=4),
                 in_=wp_raw[:, g, :, N_TILE * nt : N_TILE * (nt + 1)].rearrange(
@@ -245,7 +273,7 @@ def tile_gqa_pb_kernel(tc, q_rot, k_rot, v, Wp, out):
         def copy_qk(qi, part):
             first = H_KV * (part - 1)
             xt = qk_transposed[qi, part]
-            copy_out = nc.vector.tensor_copy if qi == 0 and part != 1 else nc.scalar.copy
+            copy_out = nc.vector.tensor_copy if (qi == 0 and part != 1) or (qi > 4 and part == 0) else nc.scalar.copy
             if part == 0:
                 copy_out(out=kT[:, :, P * qi : P * (qi + 1)], in_=xt[:])
             else:
@@ -321,7 +349,8 @@ def tile_gqa_pb_kernel(tc, q_rot, k_rot, v, Wp, out):
         def regroup_e(w):
             xt = e_transposed[w]
             grouped = ring.tile([P, 2 * K_PASS], BF16, align_bytes=64, tag="e_grouped", bufs=GROUPED_BUFS)
-            nc.scalar.copy(
+            copy_out = nc.scalar.copy if w < n_works - DRAIN else nc.vector.tensor_copy
+            copy_out(
                 out=grouped[:].bitcast(F32).rearrange("p (c q u) -> p c q u", c=2, u=2),
                 in_=xt[:].rearrange("p (c u) q -> p c q u", u=2),
             )
@@ -339,14 +368,14 @@ def tile_gqa_pb_kernel(tc, q_rot, k_rot, v, Wp, out):
             e_scales[w] = scales
 
         def e_times_v(last):
-            pv = psum_acc.tile([P, GROUP, D], F32, tag="acc")
-            for w in reversed(group_works(last)):
+            pv = psum_acc.tile([P, len(job_heads(last)), D], F32, tag="acc")
+            for w in reversed(jobs[last]):
                 lone = works[w][2] == 2
                 for c in range(2):
                     head, key0, n_keys = half_of(w, c)
                     g = key0 // K_PASS
                     nc.tensor.matmul_mx(
-                        out=pv[:, head % GROUP, :],
+                        out=pv[:, head - job_heads(last)[0], :],
                         lhsT=e_codes[w][:, c, :].bitcast(FP8X4),
                         lhsT_scale=e_scales[w][:, c, :],
                         rhs=v_codes[:, g, head // 2, :].bitcast(FP8X4),
@@ -357,23 +386,24 @@ def tile_gqa_pb_kernel(tc, q_rot, k_rot, v, Wp, out):
             pv_banks[last] = pv
 
         def invert_sums(last):
-            qi, group = tile_and_group(last)
-            heads = slice(GROUP * group, GROUP * (group + 1))
+            qi = works[last][0]
+            heads = job_heads(last)
             inverse = small.tile([P, GROUP], F32, tag="inverse")
-            nc.vector.reciprocal(out=inverse[:], in_=row_sums[qi][:, heads])
+            nc.vector.reciprocal(
+                out=inverse[:, 0 : len(heads)], in_=row_sums[qi][:, heads[0] : heads[-1] + 1]
+            )
             inverses[last] = inverse
 
         def normalise(last):
-            qi, group = tile_and_group(last)
-            heads = slice(GROUP * group, GROUP * (group + 1))
-            if group == 0:
+            qi = works[last][0]
+            heads = job_heads(last)
+            if heads[0] == 0:
                 a_tile = ring.tile([P, H, D], BF16, tag="a")
                 a_tiles[qi] = a_tile
-            inverse = inverses[last]
             nc.vector.tensor_tensor(
-                out=a_tiles[qi][:, heads, :],
+                out=a_tiles[qi][:, heads[0] : heads[-1] + 1, :],
                 in0=pv_banks[last][:],
-                in1=inverse[:].unsqueeze(2).to_broadcast([P, GROUP, D]),
+                in1=inverses[last][:, 0 : len(heads)].unsqueeze(2).to_broadcast([P, len(heads), D]),
                 op=ALU.mult,
             )
 
@@ -392,7 +422,7 @@ def tile_gqa_pb_kernel(tc, q_rot, k_rot, v, Wp, out):
         def regroup_a(last):
             qi, group = tile_and_group(last)
             xt = a_transposed[last]
-            copy_out = nc.scalar.copy if is_short(qi) else nc.vector.tensor_copy
+            copy_out = nc.scalar.copy if qi < 3 else nc.vector.tensor_copy
             copy_out(
                 out=a_grouped[qi][:, group, :].bitcast(F32).rearrange("p (q u) -> p q u", u=2),
                 in_=xt[:].rearrange("p u q -> p q u"),
@@ -430,7 +460,7 @@ def tile_gqa_pb_kernel(tc, q_rot, k_rot, v, Wp, out):
             acc = projected[qi, nt]
             cols = slice(N_TILE * nt, N_TILE * (nt + 1))
             result = ring.tile([P, N_TILE], F32, tag="result", bufs=RESULT_BUFS)
-            copy_out = nc.vector.tensor_copy if nt == 1 and not is_short(qi) else nc.scalar.copy
+            copy_out = nc.vector.tensor_copy if nt == 1 and qi in (3, 4, 7) else nc.scalar.copy
             copy_out(out=result[:], in_=acc[:])
             nc.sync.dma_start(out=out[0, P * qi : P * (qi + 1), cols], in_=result[:])
 
@@ -458,67 +488,75 @@ def tile_gqa_pb_kernel(tc, q_rot, k_rot, v, Wp, out):
         LAC, QK0, QKC, RC = LPV + 3, 2, 0, 0
         WPQ = 1
         WP0, V1, V0, WPS = 6, 19, 1, 1
+        qk_at = {}
+        for w in range(n_works):
+            qi, first_head, heads_per_work = works[w]
+            part = first_head // heads_per_work - QK_START
+            if 0 <= part < 3 and qi + 1 < Q_TILES:
+                qk_at.setdefault(w, []).append((qi + 1, part))
+        qk_at.setdefault(Q2_STEP, []).append((0, 2))
         project_at = {}
         for last in range(n_works):
             if ends_tile(last) and works[last][0] < Q_TILES - 1:
                 for nt in range(N_TILES):
-                    step = max(last + LP, 16 + N_TILES * works[last][0]) + nt
+                    step = max(last + LAG_PROJECT, WP_READY + N_TILES * works[last][0]) + nt
                     project_at.setdefault(step, []).append((works[last][0], nt))
         with tc.manual_schedule():
-            for part in range(3):
+            for part in range(2):
                 transpose_qk(0, part)
                 copy_qk(0, part)
-            for w in range(n_works + LP + N_TILES):
+            for w in range(n_works + LAG_PROJECT + N_TILES + 3):
                 if is_work(w) and works[w][1] == 0 and works[w][0] + RAW_BUFS < Q_TILES:
                     load_qk(works[w][0] + RAW_BUFS)
-                if is_work(w - LT):
-                    transpose_e(w - LT)
-                if ends_group(w - LAT):
-                    transpose_a(w - LAT)
-                if is_work(w - QK0) and works[w - QK0][1] // works[w - QK0][2] < 3 and works[w - QK0][0] + 1 < Q_TILES:
-                    transpose_qk(works[w - QK0][0] + 1, works[w - QK0][1] // works[w - QK0][2])
+                if is_work(w - LAG_TRANSPOSE):
+                    transpose_e(w - LAG_TRANSPOSE)
+                if ends_group(w - LAG_A_TRANSPOSE):
+                    transpose_a(w - LAG_A_TRANSPOSE)
+                for qi_n, part in qk_at.get(w, []):
+                    transpose_qk(qi_n, part)
                 if is_work(w):
                     scores(w, 0)
-                if ends_group(w - LPV):
-                    e_times_v(w - LPV)
+                if w - LAG_PV in jobs:
+                    e_times_v(w - LAG_PV)
                 for qi_p, nt in project_at.get(w, []):
                     project(qi_p, nt)
-                last = w - LAQ - 1
+                last = w - LAG_A_QUANTISE - 4
                 if is_work(last) and ends_group(last) and works[last][0] == Q_TILES - 1:
                     project_last_tile(tile_and_group(last)[1])
                 if is_work(w):
                     scores(w, 1)
-                if is_work(w - LM):
-                    row_max(w - LM, 0)
-                if ends_group(w - LPV):
-                    invert_sums(w - LPV)
-                if ends_group(w - LN):
-                    normalise(w - LN)
-                if is_work(w - LQ):
-                    quantise_e(w - LQ)
-                if is_work(w - LM):
-                    row_max(w - LM, 1)
-                if ends_group(w - LAQ):
-                    quantise_a(w - LAQ)
-                if is_work(w - LC):
-                    regroup_e(w - LC)
-                if ends_group(w - LAC):
-                    regroup_a(w - LAC)
-                if is_work(w - QK0 - QKC) and works[w - QK0 - QKC][1] // works[w - QK0 - QKC][2] < 3 and works[w - QK0 - QKC][0] + 1 < Q_TILES:
-                    copy_qk(works[w - QK0 - QKC][0] + 1, works[w - QK0 - QKC][1] // works[w - QK0 - QKC][2])
-                if is_work(w - LE):
-                    exponentials(w - LE)
-                if (w - WP0) % WPS == 0 and 0 <= (w - WP0) // WPS < WP_CHUNKS:
-                    regroup_wp((w - WP0) // WPS)
-                if (w - WP0 - WPQ) % WPS == 0 and 0 <= (w - WP0 - WPQ) // WPS < WP_CHUNKS:
-                    quantise_wp((w - WP0 - WPQ) // WPS)
-                if V1 <= w < V1 + H_KV // 2:
-                    prepare_v(1, w - V1)
-                if V0 <= w < V0 + H_KV // 2:
-                    prepare_v(0, w - V0)
-                for qi_p, nt in project_at.get(w - RC, []):
+                if is_work(w - LAG_ROW_MAX):
+                    row_max(w - LAG_ROW_MAX, 0)
+                if w - LAG_PV in jobs:
+                    invert_sums(w - LAG_PV)
+                if w - LAG_NORMALISE in jobs:
+                    normalise(w - LAG_NORMALISE)
+                if is_work(w - LAG_QUANTISE):
+                    quantise_e(w - LAG_QUANTISE)
+                if is_work(w - LAG_ROW_MAX):
+                    row_max(w - LAG_ROW_MAX, 1)
+                if ends_group(w - LAG_A_QUANTISE):
+                    quantise_a(w - LAG_A_QUANTISE)
+                if is_work(w - LAG_TRANSPOSE):
+                    regroup_e(w - LAG_TRANSPOSE)
+                if ends_group(w - LAG_A_TRANSPOSE):
+                    regroup_a(w - LAG_A_TRANSPOSE)
+                for qi_n, part in qk_at.get(w, []):
+                    copy_qk(qi_n, part)
+                if is_work(w - LAG_EXP):
+                    exponentials(w - LAG_EXP)
+                if w in WP_STEPS:
+                    regroup_wp(WP_STEPS.index(w))
+                if w - 1 in WP_STEPS:
+                    quantise_wp(WP_STEPS.index(w - 1))
+                for g in range(KEY_PASSES):
+                    if w in V_STEPS[g]:
+                        prepare_v(g, V_STEPS[g].index(w))
+                    if w - 1 in V_STEPS[g]:
+                        quantise_v(g, V_STEPS[g].index(w - 1))
+                for qi_p, nt in project_at.get(w, []):
                     store_result(qi_p, nt)
-                last = w - LAQ - 1
+                last = w - LAG_A_QUANTISE - 4
                 if is_work(last) and ends_tile(last) and works[last][0] == Q_TILES - 1:
                     for nt in range(N_TILES):
                         store_result(Q_TILES - 1, nt)

@@ -41,6 +41,7 @@ CODE_BUFS = 12
 LAG_ROW_MAX = 1
 LAG_EXP = 2
 LAG_TRANSPOSE = 4
+LAG_INVERT = 5
 LAG_QUANTISE = 6
 LAG_PV = 7
 LAG_NORMALISE = 8
@@ -49,11 +50,11 @@ LAG_A_QUANTISE = 11
 LAG_PROJECT = 12
 QK_START = 2
 Q2_STEP = 1
-DRAIN = 2
+DRAIN = 0
 WP_CHUNKS = C_PASSES * N_TILES
-WP_STEPS = [6, 7, 8, 10, 11, 12, 14, 15, 16]
+WP_STEPS = [6, 7, 8, 9, 10, 11, 12, 13, 14]
 V_STEPS = [[4, 5, 6], [19, 20, 21]]
-WP_READY = WP_STEPS[-1] + 2
+WP_READY = WP_STEPS[-1] + 3
 
 
 def tile_gqa_pb_kernel(tc, q_rot, k_rot, v, Wp, out):
@@ -171,6 +172,8 @@ def tile_gqa_pb_kernel(tc, q_rot, k_rot, v, Wp, out):
         )
         ident_f32 = keep.tile([P, P], F32)
         make_identity(nc, ident_f32[:])
+        minus_one = keep.tile([P, GROUP], F32)
+        nc.gpsimd.memset(minus_one[:], -1.0)
         warm_in = keep.tile([P, 1], F32)
         warm_out = keep.tile([P, 1], F32)
         nc.vector.memset(warm_in[:], 0.0)
@@ -221,12 +224,20 @@ def tile_gqa_pb_kernel(tc, q_rot, k_rot, v, Wp, out):
         last_banks = []
 
         def prepare_v(g, pair):
-            grouped = ring.tile([P, 2, D, PACK], BF16, align_bytes=64, tag="v_grouped")
+            grouped = ring.tile([P, 2, D, PACK], BF16, align_bytes=64, tag="v_grouped", bufs=3)
             for i in range(2):
-                nc.vector.tensor_copy(
-                    out=grouped[:, i, :, :],
-                    in_=v_raw[:, g, 2 * pair + i, :, :].rearrange("p t d -> p d t"),
-                )
+                rows = v_raw[:, g, 2 * pair + i, :, :].rearrange("p t d -> p d t")
+                if g == 0:
+                    nc.gpsimd.tensor_scalar(
+                        out=grouped[:, i, :, :],
+                        in0=rows,
+                        scalar1=1.0,
+                        scalar2=0.0,
+                        op0=ALU.mult,
+                        op1=ALU.add,
+                    )
+                else:
+                    nc.vector.tensor_copy(out=grouped[:, i, :, :], in_=rows)
             v_grouped[g, pair] = grouped
 
         def quantise_v(g, pair):
@@ -240,8 +251,8 @@ def tile_gqa_pb_kernel(tc, q_rot, k_rot, v, Wp, out):
 
         def regroup_wp(chunk):
             g, nt = divmod(chunk, N_TILES)
-            grouped = ring.tile([P, N_TILE, PACK], BF16, align_bytes=64, tag="wp_grouped")
-            regroup = nc.scalar.copy if nt != 1 else nc.vector.tensor_copy
+            grouped = ring.tile([P, N_TILE, PACK], BF16, align_bytes=64, tag="wp_grouped", bufs=3)
+            regroup = nc.scalar.copy if nt == 0 else nc.vector.tensor_copy
             regroup(
                 out=grouped[:].rearrange("p (c i) t -> p c t i", i=4),
                 in_=wp_raw[:, g, :, N_TILE * nt : N_TILE * (nt + 1)].rearrange(
@@ -389,8 +400,11 @@ def tile_gqa_pb_kernel(tc, q_rot, k_rot, v, Wp, out):
             qi = works[last][0]
             heads = job_heads(last)
             inverse = small.tile([P, GROUP], F32, tag="inverse")
-            nc.vector.reciprocal(
-                out=inverse[:, 0 : len(heads)], in_=row_sums[qi][:, heads[0] : heads[-1] + 1]
+            nc.gpsimd.tensor_tensor(
+                out=inverse[:, 0 : len(heads)],
+                in0=row_sums[qi][:, heads[0] : heads[-1] + 1],
+                in1=minus_one[:, 0 : len(heads)],
+                op=ALU.pow,
             )
             inverses[last] = inverse
 
@@ -460,7 +474,7 @@ def tile_gqa_pb_kernel(tc, q_rot, k_rot, v, Wp, out):
             acc = projected[qi, nt]
             cols = slice(N_TILE * nt, N_TILE * (nt + 1))
             result = ring.tile([P, N_TILE], F32, tag="result", bufs=RESULT_BUFS)
-            copy_out = nc.vector.tensor_copy if nt == 1 and qi in (3, 4, 7) else nc.scalar.copy
+            copy_out = nc.vector.tensor_copy if nt == 1 and qi == 7 else nc.scalar.copy
             copy_out(out=result[:], in_=acc[:])
             nc.sync.dma_start(out=out[0, P * qi : P * (qi + 1), cols], in_=result[:])
 
@@ -527,8 +541,8 @@ def tile_gqa_pb_kernel(tc, q_rot, k_rot, v, Wp, out):
                     scores(w, 1)
                 if is_work(w - LAG_ROW_MAX):
                     row_max(w - LAG_ROW_MAX, 0)
-                if w - LAG_PV in jobs:
-                    invert_sums(w - LAG_PV)
+                if w - LAG_INVERT in jobs:
+                    invert_sums(w - LAG_INVERT)
                 if w - LAG_NORMALISE in jobs:
                     normalise(w - LAG_NORMALISE)
                 if is_work(w - LAG_QUANTISE):
@@ -547,8 +561,8 @@ def tile_gqa_pb_kernel(tc, q_rot, k_rot, v, Wp, out):
                     exponentials(w - LAG_EXP)
                 if w in WP_STEPS:
                     regroup_wp(WP_STEPS.index(w))
-                if w - 1 in WP_STEPS:
-                    quantise_wp(WP_STEPS.index(w - 1))
+                if w - 2 in WP_STEPS:
+                    quantise_wp(WP_STEPS.index(w - 2))
                 for g in range(KEY_PASSES):
                     if w in V_STEPS[g]:
                         prepare_v(g, V_STEPS[g].index(w))

@@ -41,7 +41,6 @@ CODE_BUFS = 12
 LAG_ROW_MAX = 1
 LAG_EXP = 2
 LAG_TRANSPOSE = 4
-LAG_INVERT = 5
 LAG_QUANTISE = 6
 LAG_PV = 7
 LAG_NORMALISE = 8
@@ -50,7 +49,6 @@ LAG_A_QUANTISE = 11
 LAG_PROJECT = 12
 QK_START = 2
 Q2_STEP = 1
-DRAIN = 0
 WP_CHUNKS = C_PASSES * N_TILES
 WP_STEPS = [6, 7, 8, 9, 10, 11, 12, 13, 14]
 V_STEPS = [[4, 5, 6], [19, 20, 21]]
@@ -172,8 +170,6 @@ def tile_gqa_pb_kernel(tc, q_rot, k_rot, v, Wp, out):
         )
         ident_f32 = keep.tile([P, P], F32)
         make_identity(nc, ident_f32[:])
-        minus_one = keep.tile([P, GROUP], F32)
-        nc.gpsimd.memset(minus_one[:], -1.0)
         warm_in = keep.tile([P, 1], F32)
         warm_out = keep.tile([P, 1], F32)
         nc.vector.memset(warm_in[:], 0.0)
@@ -224,20 +220,12 @@ def tile_gqa_pb_kernel(tc, q_rot, k_rot, v, Wp, out):
         last_banks = []
 
         def prepare_v(g, pair):
-            grouped = ring.tile([P, 2, D, PACK], BF16, align_bytes=64, tag="v_grouped", bufs=3)
+            grouped = ring.tile([P, 2, D, PACK], BF16, align_bytes=64, tag="v_grouped")
             for i in range(2):
-                rows = v_raw[:, g, 2 * pair + i, :, :].rearrange("p t d -> p d t")
-                if g == 0:
-                    nc.gpsimd.tensor_scalar(
-                        out=grouped[:, i, :, :],
-                        in0=rows,
-                        scalar1=1.0,
-                        scalar2=0.0,
-                        op0=ALU.mult,
-                        op1=ALU.add,
-                    )
-                else:
-                    nc.vector.tensor_copy(out=grouped[:, i, :, :], in_=rows)
+                nc.vector.tensor_copy(
+                    out=grouped[:, i, :, :],
+                    in_=v_raw[:, g, 2 * pair + i, :, :].rearrange("p t d -> p d t"),
+                )
             v_grouped[g, pair] = grouped
 
         def quantise_v(g, pair):
@@ -360,8 +348,7 @@ def tile_gqa_pb_kernel(tc, q_rot, k_rot, v, Wp, out):
         def regroup_e(w):
             xt = e_transposed[w]
             grouped = ring.tile([P, 2 * K_PASS], BF16, align_bytes=64, tag="e_grouped", bufs=GROUPED_BUFS)
-            copy_out = nc.scalar.copy if w < n_works - DRAIN else nc.vector.tensor_copy
-            copy_out(
+            nc.scalar.copy(
                 out=grouped[:].bitcast(F32).rearrange("p (c q u) -> p c q u", c=2, u=2),
                 in_=xt[:].rearrange("p (c u) q -> p c q u", u=2),
             )
@@ -400,11 +387,8 @@ def tile_gqa_pb_kernel(tc, q_rot, k_rot, v, Wp, out):
             qi = works[last][0]
             heads = job_heads(last)
             inverse = small.tile([P, GROUP], F32, tag="inverse")
-            nc.gpsimd.tensor_tensor(
-                out=inverse[:, 0 : len(heads)],
-                in0=row_sums[qi][:, heads[0] : heads[-1] + 1],
-                in1=minus_one[:, 0 : len(heads)],
-                op=ALU.pow,
+            nc.vector.reciprocal(
+                out=inverse[:, 0 : len(heads)], in_=row_sums[qi][:, heads[0] : heads[-1] + 1]
             )
             inverses[last] = inverse
 
@@ -541,8 +525,8 @@ def tile_gqa_pb_kernel(tc, q_rot, k_rot, v, Wp, out):
                     scores(w, 1)
                 if is_work(w - LAG_ROW_MAX):
                     row_max(w - LAG_ROW_MAX, 0)
-                if w - LAG_INVERT in jobs:
-                    invert_sums(w - LAG_INVERT)
+                if w - LAG_PV in jobs:
+                    invert_sums(w - LAG_PV)
                 if w - LAG_NORMALISE in jobs:
                     normalise(w - LAG_NORMALISE)
                 if is_work(w - LAG_QUANTISE):

@@ -106,8 +106,8 @@ def tile_gqa_pb_kernel(tc, q_rot, k_rot, v, Wp, out):
         ring = stack.enter_context(tc.tile_pool(name="ring", bufs=2))
         small = stack.enter_context(tc.tile_pool(name="small", bufs=4))
         psum_s = stack.enter_context(tc.psum_pool(name="psum_s", bufs=3))
-        psum_tr = stack.enter_context(tc.psum_pool(name="psum_tr", bufs=3))
-        psum_acc = stack.enter_context(tc.psum_pool(name="psum_acc", bufs=2))
+        psum_tr = stack.enter_context(tc.psum_pool(name="psum_tr", bufs=2))
+        psum_acc = stack.enter_context(tc.psum_pool(name="psum_acc", bufs=3))
 
         q_view = q_rot[0].rearrange("h (n p) d -> n p h d", p=P)
         k_view = k_rot[0].rearrange("j (n p) d -> n p j d", p=P)
@@ -263,7 +263,7 @@ def tile_gqa_pb_kernel(tc, q_rot, k_rot, v, Wp, out):
                 qT_tile = ring.tile([P, H, P], BF16, tag="qT")
                 qT[qi] = qT_tile
             first = H_KV * (part - 1)
-            xt = psum_tr.tile([P, H_KV, P], BF16, tag="tr")
+            xt = psum_acc.tile([P, H_KV, P], BF16, tag="acc")
             for i in range(H_KV):
                 src = k_raw[qi][:, i, :] if part == 0 else q_raw[qi][:, first + i, :]
                 nc.tensor.transpose(xt[:, i, :], src, ident_bf[:])
@@ -272,7 +272,7 @@ def tile_gqa_pb_kernel(tc, q_rot, k_rot, v, Wp, out):
         def copy_qk(qi, part):
             first = H_KV * (part - 1)
             xt = qk_transposed[qi, part]
-            copy_out = nc.vector.tensor_copy if (qi == 0 and part != 1) or (qi > 4 and part == 0) else nc.scalar.copy
+            copy_out = nc.vector.tensor_copy if (qi == 0 and part != 1) or (qi > 4 and part != 2) else nc.scalar.copy
             if part == 0:
                 copy_out(out=kT[:, :, P * qi : P * (qi + 1)], in_=xt[:])
             else:
@@ -411,7 +411,7 @@ def tile_gqa_pb_kernel(tc, q_rot, k_rot, v, Wp, out):
                 grouped = ring.tile([P, C_PASSES, K_PASS], BF16, align_bytes=64, tag="a_grouped")
                 a_grouped[qi] = grouped
             a_words = a_tiles[qi][:].rearrange("p h d -> p (h d)").bitcast(F32)
-            xt = psum_tr.tile([P, 2, P], F32, tag="tr")
+            xt = psum_acc.tile([P, 2, P], F32, tag="acc")
             for u in range(2):
                 word0 = P * (2 * group + u)
                 nc.tensor.transpose(xt[:, u, :], a_words[:, word0 : word0 + P], ident_f32[:])
@@ -429,8 +429,8 @@ def tile_gqa_pb_kernel(tc, q_rot, k_rot, v, Wp, out):
         def quantise_a(last):
             qi, group = tile_and_group(last)
             if group == 0:
-                codes = ring.tile([P, C_PASSES, P], U32, align_bytes=64, tag="a_codes", bufs=4)
-                scales = ring.tile([P, C_PASSES, P], U8, align_bytes=64, tag="a_scales", bufs=4)
+                codes = ring.tile([P, C_PASSES, P], U32, align_bytes=64, tag="a_codes", bufs=5)
+                scales = ring.tile([P, C_PASSES, P], U8, align_bytes=64, tag="a_scales", bufs=5)
                 a_codes[qi] = codes
                 a_scales[qi] = scales
             nc.vector.quantize_mx(
@@ -498,6 +498,8 @@ def tile_gqa_pb_kernel(tc, q_rot, k_rot, v, Wp, out):
             if ends_tile(last) and works[last][0] < Q_TILES - 1:
                 for nt in range(N_TILES):
                     step = max(last + LAG_PROJECT, WP_READY + N_TILES * works[last][0]) + nt
+                    if works[last][0] in [6]:
+                        step = n_works + 1 + (N_TILES * [6].index(works[last][0]) + nt) // 1
                     project_at.setdefault(step, []).append((works[last][0], nt))
         with tc.manual_schedule():
             for part in range(2):

from contextlib import ExitStack
import math

import concourse.mybir as mybir
from concourse.masks import make_identity

F32 = mybir.dt.float32
BF16 = mybir.dt.bfloat16
U32 = mybir.dt.uint32
U8 = mybir.dt.uint8
FP8X4 = mybir.dt.float8_e4m3fn_x4
ALU = mybir.AluOpType
ACT = mybir.ActivationFunctionType

P = 128
PACK = 4
K_PASS = P * PACK
T = 1024
D = 128
H = 12
H_KV = 6
C = H * D
N_TILE = 512
Q_TILES = T // P
KEY_PASSES = T // K_PASS
C_PASSES = C // K_PASS
N_TILES = C // N_TILE
TILES_PER_PASS = K_PASS // P
GROUP = K_PASS // D
SCALE = 1.0 / math.sqrt(D)
MASKED = -1.0e30

FLOPS = 2 * 2 * H * (512 * 512 + 512 * 1024) * D + 2 * T * C * C

RAW_BUFS = 3
E_BUFS = 6
RESULT_BUFS = 4
SCALED_BUFS = 6
GROUPED_BUFS = 4
CODE_BUFS = 12
LAG_ROW_MAX = 1
LAG_EXP = 2
LAG_TRANSPOSE = 4
LAG_QUANTISE = 6
LAG_PV = 7
LAG_NORMALISE = 8
LAG_A_TRANSPOSE = 10
LAG_A_QUANTISE = 11
LAG_PROJECT = 12
QK_START = 2
Q2_STEP = 1
WP_CHUNKS = C_PASSES * N_TILES
WP_STEPS = [6, 7, 8, 9, 10, 11, 12, 13, 14]
V_STEPS = [[4, 5, 6], [19, 20, 21]]
WP_READY = WP_STEPS[-1] + 3


def tile_gqa_pb_kernel(tc, q_rot, k_rot, v, Wp, out):
    nc = tc.nc

    works = []
    for qi in range(Q_TILES):
        heads_per_work = 2 if qi < TILES_PER_PASS else 1
        for first_head in range(0, H, heads_per_work):
            works.append((qi, first_head, heads_per_work))
    n_works = len(works)

    def half_of(w, c):
        qi, first_head, heads_per_work = works[w]
        n_keys = P * (qi + 1)
        if heads_per_work == 2:
            return first_head + c, 0, n_keys
        return first_head, K_PASS * c, (K_PASS if c == 0 else n_keys - K_PASS)

    def is_short(qi):
        return qi < TILES_PER_PASS

    def is_work(w):
        return 0 <= w < n_works

    def ends_group(w):
        return is_work(w) and (works[w][1] + works[w][2]) % GROUP == 0

    def ends_tile(w):
        return is_work(w) and works[w][1] + works[w][2] == H

    def tile_and_group(last):
        return works[last][0], (works[last][1] + works[last][2]) // GROUP - 1

    def group_works(last):
        return range(last + 1 - GROUP // works[last][2], last + 1)

    jobs = {}
    for w in range(n_works):
        if ends_group(w):
            jobs[w] = list(group_works(w))
    jobs[n_works - 2] = jobs[n_works - 1][:-1]
    jobs[n_works - 1] = jobs[n_works - 1][-1:]

    def job_heads(last):
        first = works[jobs[last][0]][1]
        return range(first, works[last][1] + works[last][2])

    with ExitStack() as stack:
        keep = stack.enter_context(tc.tile_pool(name="keep", bufs=1))
        ring = stack.enter_context(tc.tile_pool(name="ring", bufs=2))
        small = stack.enter_context(tc.tile_pool(name="small", bufs=4))
        psum_s = stack.enter_context(tc.psum_pool(name="psum_s", bufs=3))
        psum_tr = stack.enter_context(tc.psum_pool(name="psum_tr", bufs=2))
        psum_acc = stack.enter_context(tc.psum_pool(name="psum_acc", bufs=3))

        q_view = q_rot[0].rearrange("h (n p) d -> n p h d", p=P)
        k_view = k_rot[0].rearrange("j (n p) d -> n p j d", p=P)
        v_view = v[0].rearrange("j (g u p e) d -> g u p j (e d)", g=KEY_PASSES, u=2, p=P, e=2)
        wp_view = Wp.rearrange("(g u p e) n -> g u p (e n)", g=C_PASSES, u=2, p=P, e=2)
        q_raw = {}
        k_raw = {}
        v_raw = keep.tile([P, KEY_PASSES, H_KV, PACK, D], BF16)
        wp_raw = keep.tile([P, C_PASSES, PACK, C], BF16)

        def load_q_half(qi, half):
            heads = slice(H_KV * half, H_KV * (half + 1))
            nc.sync.dma_start(out=q_raw[qi][:, heads, :], in_=q_view[qi][:, heads, :])

        def load_qk(qi, halves=(0, 1)):
            k_tile = ring.tile([P, H_KV, D], BF16, tag="k_raw", bufs=RAW_BUFS)
            nc.sync.dma_start(out=k_tile[:], in_=k_view[qi])
            k_raw[qi] = k_tile
            q_tile = ring.tile([P, H, D], BF16, tag="q_raw", bufs=RAW_BUFS)
            q_raw[qi] = q_tile
            for half in halves:
                load_q_half(qi, half)

        def load_v(g):
            for u in range(2):
                nc.sync.dma_start(
                    out=v_raw[:, g, :, 2 * u : 2 * u + 2, :].rearrange("p j e d -> p j (e d)"),
                    in_=v_view[g, u],
                )

        def load_wp(g):
            for u in range(2):
                nc.sync.dma_start(
                    out=wp_raw[:, g, 2 * u : 2 * u + 2, :].rearrange("p e n -> p (e n)"),
                    in_=wp_view[g, u],
                )

        load_qk(0, (0,))
        load_q_half(0, 1)
        load_qk(1)
        load_v(0)
        load_wp(0)
        load_qk(2)
        load_wp(1)
        load_wp(2)
        load_v(1)

        ident_bf = keep.tile([P, P], BF16)
        make_identity(nc, ident_bf[:])
        mask_bf = keep.tile([P, P], BF16)
        nc.gpsimd.memset(mask_bf[:], 0.0)
        nc.gpsimd.affine_select(
            out=mask_bf[:],
            in_=mask_bf[:],
            compare_op=ALU.is_ge,
            fill=MASKED,
            base=0,
            pattern=[[-1, P]],
            channel_multiplier=1,
        )
        ident_f32 = keep.tile([P, P], F32)
        make_identity(nc, ident_f32[:])
        warm_in = keep.tile([P, 1], F32)
        warm_out = keep.tile([P, 1], F32)
        nc.vector.memset(warm_in[:], 0.0)
        nc.scalar.activation(out=warm_out[:], in_=warm_in[:], func=ACT.Exp)

        e_tiles = []
        for block in range(2):
            row = []
            for b in range(E_BUFS):
                e_tile = keep.tile([P, 2 * K_PASS], BF16, align_bytes=64, name="e%d_%d" % (block, b))
                words = e_tile[:].rearrange("p (c k) -> p c k", c=2).bitcast(U32)
                if block == 0:
                    nc.gpsimd.memset(words[:, :, P // 2 :], 0)
                else:
                    nc.gpsimd.memset(words[:, 1:2, P // 2 :], 0)
                row.append(e_tile)
            e_tiles.append(row)

        def e_of(w):
            return e_tiles[0 if works[w][2] == 2 else 1][w % E_BUFS]

        kT = keep.tile([P, H_KV, T], BF16)
        v_codes = keep.tile([P, KEY_PASSES, H_KV, D], U32, align_bytes=64)
        v_scales = keep.tile([P, KEY_PASSES, H_KV, D], U8, align_bytes=64)
        wp_codes = keep.tile([P, C_PASSES, C], U32, align_bytes=64)
        wp_scales = keep.tile([P, C_PASSES, C], U8, align_bytes=64)

        qT = {}
        s_banks = {}
        scaled_scores = {}
        neg_max = {}
        row_sums = {}
        e_grouped = {}
        e_codes = {}
        e_scales = {}
        pv_banks = {}
        a_tiles = {}
        a_grouped = {}
        a_codes = {}
        a_scales = {}
        wp_grouped = {}
        v_grouped = {}
        inverses = {}
        e_transposed = {}
        a_transposed = {}
        qk_transposed = {}
        projected = {}
        last_banks = []

        def prepare_v(g, pair):
            grouped = ring.tile([P, 2, D, PACK], BF16, align_bytes=64, tag="v_grouped")
            for i in range(2):
                nc.vector.tensor_copy(
                    out=grouped[:, i, :, :],
                    in_=v_raw[:, g, 2 * pair + i, :, :].rearrange("p t d -> p d t"),
                )
            v_grouped[g, pair] = grouped

        def quantise_v(g, pair):
            grouped = v_grouped[g, pair]
            heads = slice(2 * pair, 2 * pair + 2)
            nc.vector.quantize_mx(
                out=v_codes[:, g, heads, :].rearrange("p j d -> p (j d)").bitcast(FP8X4),
                scales=v_scales[:, g, heads, :].rearrange("p j d -> p (j d)"),
                in_=grouped[:].rearrange("p j d t -> p (j d t)"),
            )

        def regroup_wp(chunk):
            g, nt = divmod(chunk, N_TILES)
            grouped = ring.tile([P, N_TILE, PACK], BF16, align_bytes=64, tag="wp_grouped", bufs=3)
            regroup = nc.scalar.copy if nt == 0 else nc.vector.tensor_copy
            regroup(
                out=grouped[:].rearrange("p (c i) t -> p c t i", i=4),
                in_=wp_raw[:, g, :, N_TILE * nt : N_TILE * (nt + 1)].rearrange(
                    "p t (c i) -> p c t i", i=4
                ),
            )
            wp_grouped[chunk] = grouped

        def quantise_wp(chunk):
            g, nt = divmod(chunk, N_TILES)
            cols = slice(N_TILE * nt, N_TILE * (nt + 1))
            nc.vector.quantize_mx(
                out=wp_codes[:, g, cols].bitcast(FP8X4),
                scales=wp_scales[:, g, cols],
                in_=wp_grouped[chunk][:].rearrange("p n t -> p (n t)"),
            )

        def transpose_qk(qi, part):
            if part == 0:
                qT_tile = ring.tile([P, H, P], BF16, tag="qT")
                qT[qi] = qT_tile
            first = H_KV * (part - 1)
            xt = psum_acc.tile([P, H_KV, P], BF16, tag="acc")
            for i in range(H_KV):
                src = k_raw[qi][:, i, :] if part == 0 else q_raw[qi][:, first + i, :]
                nc.tensor.transpose(xt[:, i, :], src, ident_bf[:])
            qk_transposed[qi, part] = xt

        def copy_qk(qi, part):
            first = H_KV * (part - 1)
            xt = qk_transposed[qi, part]
            copy_out = nc.vector.tensor_copy if (qi == 0 and part != 1) or (qi > 4 and part != 2) else nc.scalar.copy
            if part == 0:
                copy_out(out=kT[:, :, P * qi : P * (qi + 1)], in_=xt[:])
            else:
                copy_out(out=qT[qi][:, first : first + H_KV, :], in_=xt[:])

        def scores(w, c):
            qi = works[w][0]
            if True:
                head, key0, n_keys = half_of(w, c)
                s = psum_s.tile([P, N_TILE], F32, tag="s")
                on_diagonal = key0 + n_keys == P * (qi + 1)
                nc.tensor.matmul(
                    out=s[:, 0:n_keys],
                    lhsT=qT[qi][:, head, :],
                    rhs=kT[:, head // 2, key0 : key0 + n_keys],
                    start=True,
                    stop=not on_diagonal,
                )
                if on_diagonal:
                    nc.tensor.matmul(
                        out=s[:, n_keys - P : n_keys],
                        lhsT=ident_bf[:],
                        rhs=mask_bf[:],
                        start=False,
                        stop=True,
                    )
                s_banks[w, c] = s

        def row_max(w, c):
            if c == 0:
                scaled = ring.tile([P, 2 * N_TILE], F32, tag="scaled", bufs=SCALED_BUFS)
                bias = small.tile([P, 2], F32, tag="bias", bufs=SCALED_BUFS)
                scaled_scores[w] = scaled
                neg_max[w] = bias
            scaled = scaled_scores[w]
            bias = neg_max[w]
            if True:
                n_keys = half_of(w, c)[2]
                nc.vector.tensor_scalar(
                    out=scaled[:, N_TILE * c : N_TILE * c + n_keys],
                    in0=s_banks[w, c][:, 0:n_keys],
                    scalar1=-SCALE,
                    scalar2=bias[:, 0:1] if works[w][2] == 1 and c == 1 else None,
                    op0=ALU.mult,
                    op1=ALU.min,
                    accum_out=bias[:, c : c + 1],
                )

        def exponentials(w):
            qi, first_head, heads_per_work = works[w]
            if first_head == 0:
                sums = ring.tile([P, H], F32, tag="row_sums", bufs=3)
                row_sums[qi] = sums
            for c in range(heads_per_work):
                head = first_head + c
                cols = slice(K_PASS * c, K_PASS * c + P * (qi + 1))
                nc.scalar.activation(
                    out=e_of(w)[:, cols],
                    in_=scaled_scores[w][:, cols],
                    func=ACT.Exp,
                    bias=neg_max[w][:, 1:2] if heads_per_work == 1 else neg_max[w][:, c : c + 1],
                    scale=-1.0,
                    accum_out=row_sums[qi][:, head : head + 1],
                )

        def transpose_e(w):
            e_words = e_of(w)[:].bitcast(F32)
            xt = psum_tr.tile([P, 4, P], F32, tag="tr")
            for i in range(4):
                nc.tensor.transpose(xt[:, i, :], e_words[:, P * i : P * (i + 1)], ident_f32[:])
            e_transposed[w] = xt

        def regroup_e(w):
            xt = e_transposed[w]
            grouped = ring.tile([P, 2 * K_PASS], BF16, align_bytes=64, tag="e_grouped", bufs=GROUPED_BUFS)
            nc.scalar.copy(
                out=grouped[:].bitcast(F32).rearrange("p (c q u) -> p c q u", c=2, u=2),
                in_=xt[:].rearrange("p (c u) q -> p c q u", u=2),
            )
            e_grouped[w] = grouped

        def quantise_e(w):
            codes = ring.tile([P, 2, P], U32, align_bytes=64, tag="e_codes", bufs=CODE_BUFS)
            scales = ring.tile([P, 2, P], U8, align_bytes=64, tag="e_scales", bufs=CODE_BUFS)
            nc.vector.quantize_mx(
                out=codes[:].rearrange("p c q -> p (c q)").bitcast(FP8X4),
                scales=scales[:].rearrange("p c q -> p (c q)"),
                in_=e_grouped[w][:],
            )
            e_codes[w] = codes
            e_scales[w] = scales

        def e_times_v(last):
            pv = psum_acc.tile([P, len(job_heads(last)), D], F32, tag="acc")
            for w in reversed(jobs[last]):
                lone = works[w][2] == 2
                for c in range(2):
                    head, key0, n_keys = half_of(w, c)
                    g = key0 // K_PASS
                    nc.tensor.matmul_mx(
                        out=pv[:, head - job_heads(last)[0], :],
                        lhsT=e_codes[w][:, c, :].bitcast(FP8X4),
                        lhsT_scale=e_scales[w][:, c, :],
                        rhs=v_codes[:, g, head // 2, :].bitcast(FP8X4),
                        rhs_scale=v_scales[:, g, head // 2, :],
                        start=lone or c == 0,
                        stop=lone or c == 1,
                    )
            pv_banks[last] = pv

        def invert_sums(last):
            qi = works[last][0]
            heads = job_heads(last)
            inverse = small.tile([P, GROUP], F32, tag="inverse")
            nc.vector.reciprocal(
                out=inverse[:, 0 : len(heads)], in_=row_sums[qi][:, heads[0] : heads[-1] + 1]
            )
            inverses[last] = inverse

        def normalise(last):
            qi = works[last][0]
            heads = job_heads(last)
            if heads[0] == 0:
                a_tile = ring.tile([P, H, D], BF16, tag="a")
                a_tiles[qi] = a_tile
            nc.vector.tensor_tensor(
                out=a_tiles[qi][:, heads[0] : heads[-1] + 1, :],
                in0=pv_banks[last][:],
                in1=inverses[last][:, 0 : len(heads)].unsqueeze(2).to_broadcast([P, len(heads), D]),
                op=ALU.mult,
            )

        def transpose_a(last):
            qi, group = tile_and_group(last)
            if group == 0:
                grouped = ring.tile([P, C_PASSES, K_PASS], BF16, align_bytes=64, tag="a_grouped")
                a_grouped[qi] = grouped
            a_words = a_tiles[qi][:].rearrange("p h d -> p (h d)").bitcast(F32)
            xt = psum_acc.tile([P, 2, P], F32, tag="acc")
            for u in range(2):
                word0 = P * (2 * group + u)
                nc.tensor.transpose(xt[:, u, :], a_words[:, word0 : word0 + P], ident_f32[:])
            a_transposed[last] = xt

        def regroup_a(last):
            qi, group = tile_and_group(last)
            xt = a_transposed[last]
            copy_out = nc.scalar.copy if qi < 3 else nc.vector.tensor_copy
            copy_out(
                out=a_grouped[qi][:, group, :].bitcast(F32).rearrange("p (q u) -> p q u", u=2),
                in_=xt[:].rearrange("p u q -> p q u"),
            )

        def quantise_a(last):
            qi, group = tile_and_group(last)
            if group == 0:
                codes = ring.tile([P, C_PASSES, P], U32, align_bytes=64, tag="a_codes", bufs=5)
                scales = ring.tile([P, C_PASSES, P], U8, align_bytes=64, tag="a_scales", bufs=5)
                a_codes[qi] = codes
                a_scales[qi] = scales
            nc.vector.quantize_mx(
                out=a_codes[qi][:, group, :].bitcast(FP8X4),
                scales=a_scales[qi][:, group, :],
                in_=a_grouped[qi][:, group, :],
            )

        def project(qi, nt):
            cols = slice(N_TILE * nt, N_TILE * (nt + 1))
            acc = psum_acc.tile([P, N_TILE], F32, tag="acc")
            for g in range(C_PASSES):
                nc.tensor.matmul_mx(
                    out=acc[:],
                    lhsT=a_codes[qi][:, g, :].bitcast(FP8X4),
                    lhsT_scale=a_scales[qi][:, g, :],
                    rhs=wp_codes[:, g, cols].bitcast(FP8X4),
                    rhs_scale=wp_scales[:, g, cols],
                    start=(g == 0),
                    stop=(g == C_PASSES - 1),
                )
            projected[qi, nt] = acc

        def store_result(qi, nt):
            acc = projected[qi, nt]
            cols = slice(N_TILE * nt, N_TILE * (nt + 1))
            result = ring.tile([P, N_TILE], F32, tag="result", bufs=RESULT_BUFS)
            copy_out = nc.vector.tensor_copy if nt == 1 and qi == 7 else nc.scalar.copy
            copy_out(out=result[:], in_=acc[:])
            nc.sync.dma_start(out=out[0, P * qi : P * (qi + 1), cols], in_=result[:])

        def project_last_tile(g):
            qi = Q_TILES - 1
            for nt in range(N_TILES):
                if g == 0:
                    bank = psum_s.tile([P, N_TILE], F32, tag="s")
                    last_banks.append(bank)
                cols = slice(N_TILE * nt, N_TILE * (nt + 1))
                nc.tensor.matmul_mx(
                    out=last_banks[nt][:],
                    lhsT=a_codes[qi][:, g, :].bitcast(FP8X4),
                    lhsT_scale=a_scales[qi][:, g, :],
                    rhs=wp_codes[:, g, cols].bitcast(FP8X4),
                    rhs_scale=wp_scales[:, g, cols],
                    start=(g == 0),
                    stop=(g == C_PASSES - 1),
                )
                projected[qi, nt] = last_banks[nt]


        LE, LM, LT, LC, LQ, LPV = 2, 1, 4, 4, 6, 7
        LN, LAT, LAQ, LP = LPV + 1, LPV + 3, LPV + 4, LPV + 5
        LAC, QK0, QKC, RC = LPV + 3, 2, 0, 0
        WPQ = 1
        WP0, V1, V0, WPS = 6, 19, 1, 1
        qk_at = {}
        for w in range(n_works):
            qi, first_head, heads_per_work = works[w]
            part = first_head // heads_per_work - QK_START
            if 0 <= part < 3 and qi + 1 < Q_TILES:
                qk_at.setdefault(w, []).append((qi + 1, part))
        qk_at.setdefault(Q2_STEP, []).append((0, 2))
        project_at = {}
        for last in range(n_works):
            if ends_tile(last) and works[last][0] < Q_TILES - 1:
                for nt in range(N_TILES):
                    step = max(last + LAG_PROJECT, WP_READY + N_TILES * works[last][0]) + nt
                    if works[last][0] in [6]:
                        step = n_works + 1 + (N_TILES * [6].index(works[last][0]) + nt) // 1
                    project_at.setdefault(step, []).append((works[last][0], nt))
        with tc.manual_schedule():
            for part in range(2):
                transpose_qk(0, part)
                copy_qk(0, part)
            for w in range(n_works + LAG_PROJECT + N_TILES + 3):
                if is_work(w) and works[w][1] == 0 and works[w][0] + RAW_BUFS < Q_TILES:
                    load_qk(works[w][0] + RAW_BUFS)
                if is_work(w - LAG_TRANSPOSE):
                    transpose_e(w - LAG_TRANSPOSE)
                if ends_group(w - LAG_A_TRANSPOSE):
                    transpose_a(w - LAG_A_TRANSPOSE)
                for qi_n, part in qk_at.get(w, []):
                    transpose_qk(qi_n, part)
                if is_work(w):
                    scores(w, 0)
                if w - LAG_PV in jobs:
                    e_times_v(w - LAG_PV)
                for qi_p, nt in project_at.get(w, []):
                    project(qi_p, nt)
                last = w - LAG_A_QUANTISE - 4
                if is_work(last) and ends_group(last) and works[last][0] == Q_TILES - 1:
                    project_last_tile(tile_and_group(last)[1])
                if is_work(w):
                    scores(w, 1)
                if is_work(w - LAG_ROW_MAX):
                    row_max(w - LAG_ROW_MAX, 0)
                if w - LAG_PV in jobs:
                    invert_sums(w - LAG_PV)
                if w - LAG_NORMALISE in jobs:
                    normalise(w - LAG_NORMALISE)
                if is_work(w - LAG_QUANTISE):
                    quantise_e(w - LAG_QUANTISE)
                if is_work(w - LAG_ROW_MAX):
                    row_max(w - LAG_ROW_MAX, 1)
                if ends_group(w - LAG_A_QUANTISE):
                    quantise_a(w - LAG_A_QUANTISE)
                if is_work(w - LAG_TRANSPOSE):
                    regroup_e(w - LAG_TRANSPOSE)
                if ends_group(w - LAG_A_TRANSPOSE):
                    regroup_a(w - LAG_A_TRANSPOSE)
                for qi_n, part in qk_at.get(w, []):
                    copy_qk(qi_n, part)
                if is_work(w - LAG_EXP):
                    exponentials(w - LAG_EXP)
                if w in WP_STEPS:
                    regroup_wp(WP_STEPS.index(w))
                if w - 2 in WP_STEPS:
                    quantise_wp(WP_STEPS.index(w - 2))
                for g in range(KEY_PASSES):
                    if w in V_STEPS[g]:
                        prepare_v(g, V_STEPS[g].index(w))
                    if w - 1 in V_STEPS[g]:
                        quantise_v(g, V_STEPS[g].index(w - 1))
                for qi_p, nt in project_at.get(w, []):
                    store_result(qi_p, nt)
                last = w - LAG_A_QUANTISE - 4
                if is_work(last) and ends_tile(last) and works[last][0] == Q_TILES - 1:
                    for nt in range(N_TILES):
                        store_result(Q_TILES - 1, nt)
